import numpy as np
import ml_dtypes


def mxq(x, axis, fmt="e4m3"):
    dtype, down = {"e4m3": (ml_dtypes.float8_e4m3fn, 7), "e5m2": (ml_dtypes.float8_e5m2, 14)}[fmt]
    v = np.moveaxis(np.asarray(x, np.float32).astype(ml_dtypes.bfloat16).astype(np.float64), axis, -1)
    blocks = v.reshape(v.shape[:-1] + (-1, 32))
    amax = np.abs(blocks).max(-1, keepdims=True)
    byte = np.maximum(np.where(amax > 0, np.frexp(amax)[1] - 1 + 127, 0) - down, 1)
    scale = np.exp2(byte - 127.0)
    codes = (blocks / scale).astype(np.float32).astype(dtype).astype(np.float64)
    return np.moveaxis((codes * scale).reshape(v.shape), -1, axis)


WIDE = False


def mx_kscale(k):
    if not WIDE:
        return np.ones(k)
    levels = np.array([10, -10, 5, -5, 0])
    if k % 512:
        return np.exp2(np.random.permutation(np.resize(levels, k // 32))).repeat(32)
    a = np.empty((k // 512, 16))
    for p in range(k // 512):
        a[p, :8] = np.random.permutation(np.resize(levels, 8))
        for g in range(8):
            far = levels[np.abs(levels - a[p, g]) >= 10]
            a[p, g + 8] = far[np.random.randint(len(far))]
    return np.exp2(a.ravel()).repeat(32)


BF16 = ml_dtypes.bfloat16


def bf(x):
    return np.asarray(x, np.float32).astype(BF16)


def f64(x):
    return np.asarray(x).astype(np.float64)


B, V, H = 4096, 128, 512
G = 4 * H
EPS = 1e-5


def sigmoid(v):
    return 1.0 / (1.0 + np.exp(-v))


def layer_norm(v, w, b):
    mu = v.mean(-1, keepdims=True)
    var = ((v - mu) ** 2).mean(-1, keepdims=True)
    return (v - mu) / np.sqrt(var + EPS) * w + b


def setup_inputs():
    s = mx_kscale(H)
    return {"x": bf(np.random.standard_normal((B, V))),
            "h0": bf(np.random.standard_normal((B, H)) * s),
            "c0": bf(np.random.standard_normal((B, H))),
            "w_ih1": bf(np.random.standard_normal((G, V)) / np.sqrt(V)),
            "w_hh1": bf(np.random.standard_normal((G, H)) / np.sqrt(H) / s),
            "lni_w1": bf(1.0 + 0.1 * np.random.standard_normal(G)),
            "lni_b1": bf(0.1 * np.random.standard_normal(G)),
            "lnh_w1": bf(1.0 + 0.1 * np.random.standard_normal(G)),
            "lnh_b1": bf(0.1 * np.random.standard_normal(G)),
            "lnc_w1": bf(1.0 + 0.1 * np.random.standard_normal(H)),
            "lnc_b1": bf(0.1 * np.random.standard_normal(H))}


def reference(x, h0, c0, w_ih1, w_hh1, lni_w1, lni_b1, lnh_w1, lnh_b1, lnc_w1, lnc_b1):
    a = f64(x) @ f64(w_ih1).T
    r = mxq(f64(h0), 1, "e4m3") @ mxq(f64(w_hh1), 1, "e4m3").T
    gates = layer_norm(a, f64(lni_w1), f64(lni_b1)) + layer_norm(r, f64(lnh_w1), f64(lnh_b1))
    i, f, g, o = np.split(gates, 4, axis=1)
    cy = layer_norm(sigmoid(f) * f64(c0) + sigmoid(i) * np.tanh(g), f64(lnc_w1), f64(lnc_b1))
    hy = sigmoid(o) * np.tanh(cy)
    return hy, cy

@@ -1,0 +1,543 @@
+from contextlib import ExitStack
+
+import concourse.mybir as mybir
+from concourse.masks import make_identity
+
+F32 = mybir.dt.float32
+BF16 = mybir.dt.bfloat16
+U32 = mybir.dt.uint32
+U8 = mybir.dt.uint8
+FP8X4 = mybir.dt.float8_e4m3fn_x4
+ALU = mybir.AluOpType
+ACT = mybir.ActivationFunctionType
+AX = mybir.AxisListType
+
+P = 128
+B, V, H = 4096, 128, 512
+G = 4 * H
+NT = B // P
+ST = 4
+EPS = 1e-5
+FLOPS = 2 * B * G * (H + V)
+
+RAW_BUFS = 5
+GROUPED_BUFS = 5
+
+C1_BUFS = 6
+C2_BUFS = 3
+LAST_SLOT = NT + 1
+
+
+def CELL_PLAN():
+    plan = {}
+
+    def put(n, i, name, t, on_vector=False):
+        if (n, i) not in plan:
+            plan[(n, i)] = []
+        plan[(n, i)].append((name, t, on_vector))
+
+    for t in range(NT - 2 * ST):
+        put(t + 4, 0, "c1", t)
+        put(t + 4, 0, "c2", t)
+        if t % 2 in (1,):
+            put(t + 4, 3, "cs1", t)
+            put(t + 5, 0, "cs2", t)
+        else:
+            put(t + 5, 0, "cstat", t)
+        put(t + 5, 1, "cpow", t)
+        put(t + 4, 1, "csum", t)
+        put(t + 5, 1, "y", t)
+        put(t + 5, 2, "cy", t)
+        put(t + 6, 2, "hy", t)
+        put(t + 5, 3, "th", t)
+    for j, t in enumerate(range(NT - 2 * ST, NT - ST)):
+        n = NT - ST + j // 2
+        v = j % 2 == 1
+        put(n, 0 + v, "c1", t, v)
+        put(n, 0 + v, "c2", t, v)
+        put(n, 1 + v, "csum", t, v)
+        put(n + 1, 0 + v, "cstat", t)
+        put(n + 1, 1 + v, "cpow", t)
+        put(n + 1, 1 + v, "y", t)
+        put(n + 1, 2 + v, "cy", t)
+        put(n + 2, 0 + v, "th", t)
+        put(n + 2, 2 + v, "hy", t, True)
+    for j, t in enumerate(range(NT - ST, NT)):
+        m = 4 * (NT - 1) + j
+        put((m - 2) // 4, (m - 2) % 4, "c1", t)
+        for d, names in ((1, ("c2", "csum", "cstat")), (2, ("cpow", "y")), (3, ("cy",)), (4, ("th",)), (5, ("hy",))):
+            for name in names:
+                put((m + d) // 4, (m + d) % 4, name, t, True)
+    return plan
+
+
+def tile_multilstm_pa_t_kernel(
+    tc, x, h0, c0, w_ih1, w_hh1, lni_w1, lni_b1, lnh_w1, lnh_b1, lnc_w1, lnc_b1, out_0, out_1
+):
+    nc = tc.nc
+    x_v = x.rearrange("(p t) v -> p t v", t=NT)
+    h0_v = h0.rearrange("(p t) k -> p t k", t=NT)
+    c0_v = c0.rearrange("(p t) k -> p t k", t=NT)
+    hy_v = out_0.rearrange("(p t) k -> p t k", t=NT)
+    cy_v = out_1.rearrange("(p t) k -> p t k", t=NT)
+    whh_v = w_hh1.rearrange("(t p) k -> p t k", p=P)
+    wih_v = w_ih1.rearrange("(t p) v -> p t v", p=P)
+
+    with ExitStack() as ctx:
+        const = ctx.enter_context(tc.tile_pool(name="const", bufs=1))
+        small = ctx.enter_context(tc.tile_pool(name="small", bufs=2))
+        gates = ctx.enter_context(tc.tile_pool(name="gates", bufs=9))
+        work = ctx.enter_context(tc.tile_pool(name="work", bufs=2))
+        psum = ctx.enter_context(tc.psum_pool(name="psum", bufs=4))
+        cellp = []
+
+        ident_f = const.tile([P, P], F32, name="ident_f")
+        make_identity(nc, ident_f[:])
+        ident_b = const.tile([P, P], BF16, name="ident_b")
+        make_identity(nc, ident_b[:])
+        mhalf = const.tile([P, NT], F32, name="mhalf")
+        nc.vector.memset(mhalf[:], -0.5)
+        ones_b = const.tile([P, 2], BF16, name="ones_b")
+        nc.vector.memset(ones_b[:], 1.0)
+
+        w_codes = const.tile([P, G], U32, name="w_codes", align_bytes=64)
+        w_scales = const.tile([P, G], U8, name="w_scales", align_bytes=64)
+        h_codes = const.tile([P, B], U32, name="h_codes", align_bytes=64)
+        h_scales = const.tile([P, B], U8, name="h_scales", align_bytes=64)
+        x_t = const.tile([P, B], BF16, name="x_t")
+        w_t = const.tile([P, G], BF16, name="w_t")
+        wh_bc = const.tile([P, G], BF16, name="wh_bc")
+        cw_bc = const.tile([P, H], BF16, name="cw_bc")
+        cb_bc = const.tile([P, H], BF16, name="cb_bc")
+        g_hl = const.tile([P, 2, P + 2], BF16, name="g_hl")
+        v_t = const.tile([P, 48], F32, name="v_t")
+        b_t = const.tile([P, 16], F32, name="b_t")
+        sum_a = const.tile([P, NT], F32, name="sum_a")
+        sumsq_a = const.tile([P, NT], F32, name="sumsq_a")
+        mu_a = const.tile([P, NT], F32, name="mu_a")
+        musq_a = const.tile([P, NT], F32, name="musq_a")
+        var_a = const.tile([P, NT], F32, name="var_a")
+        ve_a = const.tile([P, NT], F32, name="ve_a")
+        rs_a = const.tile([P, NT], F32, name="rs_a")
+        nb_a = const.tile([P, NT], F32, name="nb_a")
+
+        s_bank, q_bank, st_r, a_bank, t_bank, p_bank = {}, {}, {}, {}, {}, {}
+        gt, so, mv_r, rs_r, ahat, p2t, c0s = {}, {}, {}, {}, {}, {}, {}
+        c1s, c2s, ys, cys, tcs, mv_c, rs_c = {}, {}, {}, {}, {}, {}, {}
+        nmu_c, var_c = {}, {}
+
+        def inside(i):
+            return 0 <= i < NT
+
+        def rsqrt_eps(var, tag, bufs):
+            ve = small.tile([P, 1], F32, name="ve_" + tag, tag="ve_" + tag)
+            nc.gpsimd.tensor_scalar(out=ve[:], in0=var, scalar1=EPS, scalar2=1.0, op0=ALU.add, op1=ALU.mult)
+            rs = small.tile([P, 1], F32, name="rs_" + tag, tag="rs_" + tag, bufs=bufs)
+            nc.gpsimd.tensor_tensor(out=rs[:], in0=ve[:], in1=mhalf[:, 0:1], op=ALU.pow)
+            return rs
+
+        def r_pass(t, c):
+            rows = slice(t * P, (t + 1) * P)
+            cols = slice(c * H, (c + 1) * H)
+            bank = psum.tile([P, H], F32, name="r_ps", tag="vs", bufs=4)
+            nc.tensor.matmul_mx(
+                out=bank[:],
+                lhsT=h_codes[:, rows].bitcast(FP8X4),
+                lhsT_scale=h_scales[:, rows],
+                rhs=w_codes[:, cols].bitcast(FP8X4),
+                rhs_scale=w_scales[:, cols],
+                start=True,
+                stop=True,
+            )
+            return bank
+
+        def fill_st(t, c):
+            if inside(t):
+                s_bank[(t, c)] = r_pass(t, c)
+
+        def fill_q(t, c):
+            if inside(t):
+                q_bank[(t, c)] = r_pass(t, c)
+
+        def rd_st(t, c):
+            if not inside(t):
+                return
+            if c == 0:
+                st_r[t] = small.tile([P, 4, 6], F32, name="st_r", tag="st_r")
+            nc.vector.bn_stats(out=st_r[t][:, c, :], in_=s_bank[(t, c)][:])
+
+        def aggr(t):
+            if not inside(t):
+                return
+            mv = small.tile([P, 2], F32, name="mv_r", tag="mv_r", bufs=3)
+            nc.vector.bn_aggr(out=mv[:], in_=st_r[t][:].rearrange("p c s -> p (c s)"))
+            mv_r[t] = mv
+            rs_r[t] = rsqrt_eps(mv[:, 1:2], "r", 11)
+
+        def rd_q(t, c):
+            if not inside(t):
+                return
+            if c == 0:
+                gt[t] = gates.tile([P, G], F32, name="gate", tag="gate")
+            cols = slice(c * H, (c + 1) * H)
+            nc.vector.scalar_tensor_tensor(
+                out=gt[t][:, cols],
+                in0=q_bank[(t, c)][:],
+                scalar=mv_r[t][:, 0:1],
+                in1=wh_bc[:, cols],
+                op0=ALU.subtract,
+                op1=ALU.mult,
+            )
+
+        def am(k, bt):
+            if not inside(k):
+                return
+            s, c = divmod(k, 4)
+            t = ST * s + bt
+            bank = psum.tile([P, H], F32, name="a_ps", tag="ss", bufs=4)
+            nc.tensor.matmul(
+                bank[:], lhsT=x_t[:, t * P:(t + 1) * P], rhs=w_t[:, c * H:(c + 1) * H], start=True, stop=True
+            )
+            a_bank[(k, bt)] = bank
+
+        def ah(k, bt):
+            if not inside(k):
+                return
+            t = ST * (k // 4) + bt
+            if bt == 0:
+                ahat[k] = work.tile([P, ST, H], F32, name="ahat", tag="ahat")
+            nc.scalar.activation(
+                out=ahat[k][:, bt, :],
+                in_=a_bank[(k, bt)][:],
+                func=ACT.Identity,
+                bias=nb_a[:, t:t + 1],
+                scale=rs_a[:, t:t + 1],
+            )
+
+        def tb(k, jb):
+            if not inside(k):
+                return
+            bank = psum.tile([P, ST, P], F32, name="t_ps", tag="ss", bufs=4)
+            for bt in range(ST):
+                nc.tensor.transpose(bank[:, bt, :], ahat[k][:, bt, jb * P:(jb + 1) * P], ident_f[:])
+            t_bank[(k, jb)] = bank
+
+        def pt(k, jb):
+            if not inside(k):
+                return
+            if jb == 0:
+                p2t[k] = work.tile([P, 4, ST * P], F32, name="p2t", tag="p2t")
+            col = 4 * (k % 4) + jb
+            nc.scalar.activation(
+                out=p2t[k][:, jb, :],
+                in_=t_bank[(k, jb)][:].rearrange("p t b -> p (t b)"),
+                func=ACT.Identity,
+                bias=b_t[:, col:col + 1],
+                scale=v_t[:, col:col + 1],
+            )
+
+        def p2(k, bt):
+            if not inside(k):
+                return
+            bank = psum.tile([P, 4, P], F32, name="p_ps", tag="vs", bufs=4)
+            for jb in range(4):
+                nc.tensor.transpose(bank[:, jb, :], p2t[k][:, jb, bt * P:(bt + 1) * P], ident_f[:])
+            p_bank[(k, bt)] = bank
+
+        def z(k, bt):
+            if not inside(k):
+                return
+            s, c = divmod(k, 4)
+            t = ST * s + bt
+            dst = gt[t][:, c * H:(c + 1) * H]
+            nc.vector.scalar_tensor_tensor(
+                out=dst,
+                in0=dst,
+                scalar=rs_r[t][:, 0:1],
+                in1=p_bank[(k, bt)][:].rearrange("p j c -> p (j c)"),
+                op0=ALU.mult,
+                op1=ALU.add,
+            )
+
+        def act(k, bt):
+            if not inside(k):
+                return
+            s, c = divmod(k, 4)
+            t = ST * s + bt
+            src = gt[t][:, c * H:(c + 1) * H]
+            if c == 3:
+                so[t] = cellp[0].tile([P, H], F32, name="so", tag="so", bufs=8)
+                nc.scalar.activation(out=so[t][:], in_=src, func=ACT.Sigmoid)
+            else:
+                nc.scalar.activation(out=src, in_=src, func=(ACT.Tanh if c == 2 else ACT.Sigmoid))
+
+        def c1op(t, eng):
+            s, bt = divmod(t, ST)
+            c1s[t] = cellp[0].tile([P, H], F32, name="c1", tag="c1", bufs=C1_BUFS)
+            eng.tensor_tensor(out=c1s[t][:], in0=gt[t][:, H:2 * H], in1=c0s[s][:, bt, :], op=ALU.mult)
+
+        def c2op(t, eng):
+            c2s[t] = cellp[0].tile([P, H], F32, name="c2", tag="c2", bufs=C2_BUFS)
+            eng.tensor_tensor(out=c2s[t][:], in0=gt[t][:, 0:H], in1=gt[t][:, 2 * H:3 * H], op=ALU.mult)
+
+        def csum(t, eng):
+            eng.tensor_tensor(out=c1s[t][:], in0=c1s[t][:], in1=c2s[t][:], op=ALU.add)
+
+        def cstat(t):
+            if not inside(t):
+                return
+            st6 = small.tile([P, 6], F32, name="st_c", tag="st_c")
+            nc.vector.bn_stats(out=st6[:], in_=c1s[t][:])
+            mv = small.tile([P, 2], F32, name="mv_c", tag="mv_c", bufs=3)
+            nc.vector.bn_aggr(out=mv[:], in_=st6[:])
+            mv_c[t] = mv
+
+        def cs1(t):
+            junk = small.tile([P, H], BF16, name="junk_c", tag="junk_c")
+            total = small.tile([P, 1], F32, name="sum_c", tag="sum_c")
+            nc.scalar.activation(out=junk[:], in_=c1s[t][:], func=ACT.Identity, accum_out=total[:])
+            nmu_c[t] = small.tile([P, 1], F32, name="nmu_c", tag="nmu_c", bufs=3)
+            nc.scalar.activation(out=nmu_c[t][:], in_=total[:], func=ACT.Identity, scale=-1.0 / H)
+
+        def cs2(t):
+            junk = small.tile([P, H], BF16, name="junk_c", tag="junk_c")
+            ssq = small.tile([P, 1], F32, name="ssq_c", tag="ssq_c")
+            nc.scalar.activation(out=junk[:], in_=c1s[t][:], func=ACT.Square, bias=nmu_c[t][:, 0:1], accum_out=ssq[:])
+            var_c[t] = small.tile([P, 1], F32, name="var_c", tag="var_c", bufs=3)
+            nc.scalar.activation(out=var_c[t][:], in_=ssq[:], func=ACT.Identity, scale=1.0 / H)
+
+        def cpow(t):
+            if not inside(t):
+                return
+            rs_c[t] = rsqrt_eps(var_c[t][:, 0:1] if t in var_c else mv_c[t][:, 1:2], "c", 3)
+
+        def yop(t):
+            if not inside(t):
+                return
+            ys[t] = cellp[0].tile([P, H], F32, name="y", tag="y")
+            nc.vector.scalar_tensor_tensor(
+                out=ys[t][:],
+                in0=c1s[t][:],
+                scalar=(nmu_c[t][:, 0:1] if t in nmu_c else mv_c[t][:, 0:1]),
+                in1=cw_bc[:],
+                op0=(ALU.add if t in nmu_c else ALU.subtract),
+                op1=ALU.mult,
+            )
+
+        def cyop(t):
+            if not inside(t):
+                return
+            cys[t] = cellp[0].tile([P, H], F32, name="cy", tag="cy", bufs=3)
+            nc.vector.scalar_tensor_tensor(
+                out=cys[t][:], in0=ys[t][:], scalar=rs_c[t][:, 0:1], in1=cb_bc[:], op0=ALU.mult, op1=ALU.add
+            )
+            nc.sync.dma_start(out=cy_v[:, t, :], in_=cys[t][:])
+
+        def th(t):
+            if not inside(t):
+                return
+            tcs[t] = cellp[0].tile([P, H], F32, name="tcy", tag="tcy", bufs=3)
+            nc.scalar.activation(out=tcs[t][:], in_=cys[t][:], func=ACT.Tanh)
+
+        def hyop(t, eng):
+            hy = cellp[0].tile([P, H], F32, name="hy", tag="hy", bufs=4)
+            eng.tensor_tensor(out=hy[:], in0=so[t][:], in1=tcs[t][:], op=ALU.mult)
+            nc.sync.dma_start(out=hy_v[:, t, :], in_=hy[:])
+
+
+        two_input = {"c1": c1op, "c2": c2op, "csum": csum, "hy": hyop}
+        one_engine = {"cstat": cstat, "cpow": cpow, "y": yop, "cy": cyop, "th": th, "cs1": cs1, "cs2": cs2}
+        plan = CELL_PLAN()
+
+        def slot(n, prep):
+            if n % ST == 0 and inside(n):
+                c0s[n // ST] = work.tile([P, ST, H], BF16, name="c0_sb", tag="c0_sb", bufs=3)
+                nc.sync.dma_start(out=c0s[n // ST][:], in_=c0_v[:, n:n + ST, :])
+            for i in range(4):
+                n1, i1 = divmod(4 * n + i + 1, 4)
+                n2, i2 = divmod(4 * n + i + 2, 4)
+                ah(n + 2, i)
+                tb(n1 + 1, i1)
+                pt(n + 1, i)
+                am(n2 + 2, i2)
+                act(n - 1, i)
+                fill_st(n1 + 5, i1)
+                rd_st(n + 5, i)
+                fill_q(n1 + 4, i1)
+                rd_q(n + 4, i)
+                p2(n1, i1)
+                z(n, i)
+                for name, t, on_vector in plan.get((n, i), []):
+                    if name in two_input:
+                        two_input[name](t, nc.vector if on_vector else nc.gpsimd)
+                    else:
+                        one_engine[name](t)
+                if i == 3:
+                    aggr(n + 5)
+                for job in prep.get((n, i), []):
+                    job()
+
+        with tc.tile_pool(name="pro", bufs=1) as pro, tc.tile_pool(name="stage", bufs=2) as stg:
+            x_sb = pro.tile([P, NT, V], BF16, name="x_sb")
+            w_n = pro.tile([P, 16, V], BF16, name="w_n")
+            vec = pro.tile([P, P], BF16, name="vec")
+            nc.vector.memset(vec[:], 0.0)
+
+            raws = {}
+            groupeds = {}
+            y_bank = {}
+
+            def load_rows(j):
+                if 1 <= j <= 4:
+                    src = whh_v[:, ST * (j - 1):ST * j, :]
+                else:
+                    s = max(j - 4, 0)
+                    src = h0_v[:, ST * s:ST * (s + 1), :]
+                raws[j] = stg.tile([P, ST * H], BF16, name="raw", tag="raw", bufs=RAW_BUFS)
+                nc.sync.dma_start(out=raws[j][:].rearrange("p (t k) -> p t k", t=ST), in_=src)
+
+            def pack_rows(j):
+                words = raws[j][:].bitcast(F32)
+                grouped = stg.tile([P, ST * P * 4], BF16, name="grouped", tag="grouped", bufs=GROUPED_BUFS, align_bytes=64)
+                groupeds[j] = grouped
+                g_words = grouped[:].bitcast(F32).rearrange("p (t c u) -> p t c u", t=ST, u=2)
+                for half in range(2):
+                    bank = psum.tile([P, 2, 2, P], F32, name="tp_w", tag="ss")
+                    for i in range(2):
+                        for u in range(2):
+                            first = (2 * half + i) * (H // 2)
+                            nc.tensor.transpose(bank[:, i, u, :], words[:, first + u:first + H // 2:2], ident_f[:])
+                    nc.scalar.copy(
+                        out=g_words[:, 2 * half:2 * half + 2, :, :], in_=bank[:].rearrange("p t u c -> p t c u")
+                    )
+                if j + RAW_BUFS < 12:
+                    load_rows(j + RAW_BUFS)
+
+            def quant_rows(j):
+                is_w = 1 <= j <= 4
+                first = (j - 1 if is_w else max(j - 4, 0)) * H
+                cols = slice(first, first + H)
+                codes = w_codes[:, cols] if is_w else h_codes[:, cols]
+                scales = w_scales[:, cols] if is_w else h_scales[:, cols]
+                nc.vector.quantize_mx(out=codes.bitcast(FP8X4), scales=scales, in_=groupeds[j][:])
+
+            def vec_t():
+                bank = psum.tile([P, P], BF16, name="tp_v", tag="vs")
+                nc.tensor.transpose(bank[:], vec[:], ident_b[:])
+                nc.vector.tensor_copy(out=v_t[:], in_=bank[:, 0:48])
+                nc.vector.tensor_tensor(out=b_t[:], in0=v_t[:, 16:32], in1=v_t[:, 32:48], op=ALU.add)
+
+            def flip(dst, src, g):
+                bank = psum.tile([P, 4, P], BF16, name="tp_b", tag="ss")
+                for i in range(4):
+                    nc.tensor.transpose(bank[:, i, :], src[:, 4 * g + i, :], ident_b[:])
+                nc.scalar.copy(out=dst[:, 4 * g * P:4 * (g + 1) * P], in_=bank[:].rearrange("p t c -> p (t c)"))
+
+            def gram():
+                g_ps = psum.tile([P, P + 2], F32, name="g_ps", tag="vs")
+                for t in range(16):
+                    nc.tensor.matmul(
+                        g_ps[:, 0:P], lhsT=w_n[:, t, :], rhs=w_n[:, t, :], start=(t == 0), stop=(t == 15)
+                    )
+                for t in range(16):
+                    nc.tensor.matmul(
+                        g_ps[:, P:P + 2], lhsT=w_n[:, t, :], rhs=ones_b[:], start=(t == 0), stop=(t == 15)
+                    )
+                nc.vector.tensor_copy(out=g_hl[:, 0, :], in_=g_ps[:])
+                nc.vector.tensor_tensor(out=g_hl[:, 1, :], in0=g_ps[:], in1=g_hl[:, 0, :], op=ALU.subtract)
+
+            def a_mm(t0):
+                y_ps = psum.tile([P, 2, P + 2], F32, name="y_ps", tag="ss")
+                for i in range(2):
+                    lhs = x_t[:, (t0 + i) * P:(t0 + i + 1) * P]
+                    nc.tensor.matmul(y_ps[:, i, :], lhsT=lhs, rhs=g_hl[:, 0, :], start=True, stop=False)
+                    nc.tensor.matmul(y_ps[:, i, :], lhsT=lhs, rhs=g_hl[:, 1, :], start=False, stop=True)
+                y_bank[t0] = y_ps
+
+            def a_red(t0):
+                y_ps = y_bank[t0]
+                for i in range(2):
+                    junk = pro.tile([P, P], F32, name="junk", tag="junk", bufs=2)
+                    nc.vector.scalar_tensor_tensor(
+                        out=junk[:],
+                        in0=y_ps[:, i, 0:P],
+                        scalar=1.0,
+                        in1=x_sb[:, t0 + i, :],
+                        op0=ALU.mult,
+                        op1=ALU.mult,
+                        accum_out=sumsq_a[:, t0 + i:t0 + i + 1],
+                    )
+                nc.vector.tensor_copy(out=sum_a[:, t0:t0 + 2], in_=y_ps[:, :, P])
+
+            def a_finish(lo, hi):
+                c = slice(lo, hi)
+                nc.vector.tensor_scalar(out=mu_a[:, c], in0=sum_a[:, c], scalar1=1.0 / G, scalar2=None, op0=ALU.mult)
+                nc.vector.tensor_tensor(out=musq_a[:, c], in0=mu_a[:, c], in1=mu_a[:, c], op=ALU.mult)
+                nc.vector.scalar_tensor_tensor(
+                    out=var_a[:, c], in0=sumsq_a[:, c], scalar=1.0 / G, in1=musq_a[:, c], op0=ALU.mult, op1=ALU.subtract
+                )
+                nc.vector.tensor_scalar(
+                    out=ve_a[:, c], in0=var_a[:, c], scalar1=0.0, scalar2=EPS, op0=ALU.max, op1=ALU.add
+                )
+                nc.gpsimd.tensor_tensor(out=rs_a[:, c], in0=ve_a[:, c], in1=mhalf[:, c], op=ALU.pow)
+
+            def a_bias(lo, hi):
+                c = slice(lo, hi)
+                nc.vector.scalar_tensor_tensor(
+                    out=nb_a[:, c], in0=mu_a[:, c], scalar=-1.0, in1=rs_a[:, c], op0=ALU.mult, op1=ALU.mult
+                )
+
+            rows_b = pro.tile([P, G + 2 * H], BF16, name="rows_b")
+            nc.vector.memset(rows_b[:], 0.0)
+            ones_sq = pro.tile([P, P], BF16, name="ones_sq")
+            nc.vector.memset(ones_sq[:], 1.0)
+
+            def spread(dst, first):
+                bank = psum.tile([P, H], F32, name="b_ps", tag="ss")
+                nc.tensor.matmul(bank[:], lhsT=ones_sq[:], rhs=rows_b[:, first:first + H], start=True, stop=True)
+                nc.scalar.copy(out=dst, in_=bank[:])
+
+            for j in range(RAW_BUFS):
+                load_rows(j)
+            nc.sync.dma_start(out=rows_b[0:1, 0:G], in_=lnh_w1.rearrange("(o g) -> o g", o=1))
+            nc.sync.dma_start(out=rows_b[0:1, G:G + H], in_=lnc_w1.rearrange("(o g) -> o g", o=1))
+            nc.sync.dma_start(out=rows_b[0:1, G + H:G + 2 * H], in_=lnc_b1.rearrange("(o g) -> o g", o=1))
+            nc.sync.dma_start(out=w_n[:], in_=wih_v)
+            nc.sync.dma_start(out=x_sb[:], in_=x_v)
+            for j in range(5):
+                pack_rows(j)
+                quant_rows(j)
+            for c in range(4):
+                spread(wh_bc[:, c * H:(c + 1) * H], c * H)
+            nc.sync.dma_start(out=vec[0:16, :], in_=lni_w1.rearrange("(t p) -> t p", p=P))
+            nc.sync.dma_start(out=vec[16:32, :], in_=lni_b1.rearrange("(t p) -> t p", p=P))
+            nc.sync.dma_start(out=vec[32:48, :], in_=lnh_b1.rearrange("(t p) -> t p", p=P))
+            flip(w_t, w_n, 0)
+            flip(x_t, x_sb, 0)
+            gram()
+            for t0 in (0, 2):
+                a_mm(t0)
+                a_red(t0)
+            a_finish(0, 4)
+            a_bias(0, 4)
+            vec_t()
+            pack_rows(5)
+            quant_rows(5)
+            for g in range(1, 4):
+                flip(w_t, w_n, g)
+            for g in range(1, 8):
+                flip(x_t, x_sb, g)
+                for t0 in (4 * g, 4 * g + 2):
+                    a_mm(t0)
+                    a_red(t0)
+            a_finish(4, NT)
+            a_bias(4, NT)
+            spread(cw_bc[:], G)
+            spread(cb_bc[:], G + H)
+            for j in range(6, 12):
+                pack_rows(j)
+                quant_rows(j)
+        cellp.append(ctx.enter_context(tc.tile_pool(name="cellp", bufs=2)))
+        with tc.manual_schedule():
+            for n in range(-6, LAST_SLOT + 1):
+                slot(n, {})

@@ -10,7 +10,6 @@ U8 = mybir.dt.uint8
 FP8X4 = mybir.dt.float8_e4m3fn_x4
 ALU = mybir.AluOpType
 ACT = mybir.ActivationFunctionType
-AX = mybir.AxisListType
 
 P = 128
 B, V, H = 4096, 128, 512
@@ -19,56 +18,9 @@ NT = B // P
 ST = 4
 EPS = 1e-5
 FLOPS = 2 * B * G * (H + V)
-
-RAW_BUFS = 5
-GROUPED_BUFS = 5
-
-C1_BUFS = 6
-C2_BUFS = 3
-LAST_SLOT = NT + 1
-
-
-def CELL_PLAN():
-    plan = {}
-
-    def put(n, i, name, t, on_vector=False):
-        if (n, i) not in plan:
-            plan[(n, i)] = []
-        plan[(n, i)].append((name, t, on_vector))
-
-    for t in range(NT - 2 * ST):
-        put(t + 4, 0, "c1", t)
-        put(t + 4, 0, "c2", t)
-        if t % 2 in (1,):
-            put(t + 4, 3, "cs1", t)
-            put(t + 5, 0, "cs2", t)
-        else:
-            put(t + 5, 0, "cstat", t)
-        put(t + 5, 1, "cpow", t)
-        put(t + 4, 1, "csum", t)
-        put(t + 5, 1, "y", t)
-        put(t + 5, 2, "cy", t)
-        put(t + 6, 2, "hy", t)
-        put(t + 5, 3, "th", t)
-    for j, t in enumerate(range(NT - 2 * ST, NT - ST)):
-        n = NT - ST + j // 2
-        v = j % 2 == 1
-        put(n, 0 + v, "c1", t, v)
-        put(n, 0 + v, "c2", t, v)
-        put(n, 1 + v, "csum", t, v)
-        put(n + 1, 0 + v, "cstat", t)
-        put(n + 1, 1 + v, "cpow", t)
-        put(n + 1, 1 + v, "y", t)
-        put(n + 1, 2 + v, "cy", t)
-        put(n + 2, 0 + v, "th", t)
-        put(n + 2, 2 + v, "hy", t, True)
-    for j, t in enumerate(range(NT - ST, NT)):
-        m = 4 * (NT - 1) + j
-        put((m - 2) // 4, (m - 2) % 4, "c1", t)
-        for d, names in ((1, ("c2", "csum", "cstat")), (2, ("cpow", "y")), (3, ("cy",)), (4, ("th",)), (5, ("hy",))):
-            for name in names:
-                put((m + d) // 4, (m + d) % 4, name, t, True)
-    return plan
+CHUNK_ORDER = (1, 0, 2, 3)
+LEAD = 1
+DEPTH = 3
 
 
 def tile_multilstm_pa_t_kernel(
@@ -86,10 +38,8 @@ def tile_multilstm_pa_t_kernel(
     with ExitStack() as ctx:
         const = ctx.enter_context(tc.tile_pool(name="const", bufs=1))
         small = ctx.enter_context(tc.tile_pool(name="small", bufs=2))
-        gates = ctx.enter_context(tc.tile_pool(name="gates", bufs=9))
         work = ctx.enter_context(tc.tile_pool(name="work", bufs=2))
         psum = ctx.enter_context(tc.psum_pool(name="psum", bufs=4))
-        cellp = []
 
         ident_f = const.tile([P, P], F32, name="ident_f")
         make_identity(nc, ident_f[:])
@@ -99,16 +49,17 @@ def tile_multilstm_pa_t_kernel(
         nc.vector.memset(mhalf[:], -0.5)
         ones_b = const.tile([P, 2], BF16, name="ones_b")
         nc.vector.memset(ones_b[:], 1.0)
+        ones_sq = const.tile([P, P], BF16, name="ones_sq")
+        nc.vector.memset(ones_sq[:], 1.0)
 
         w_codes = const.tile([P, G], U32, name="w_codes", align_bytes=64)
         w_scales = const.tile([P, G], U8, name="w_scales", align_bytes=64)
         h_codes = const.tile([P, B], U32, name="h_codes", align_bytes=64)
         h_scales = const.tile([P, B], U8, name="h_scales", align_bytes=64)
         x_t = const.tile([P, B], BF16, name="x_t")
-        w_t = const.tile([P, G], BF16, name="w_t")
+        x_f = const.tile([P, B], F32, name="x_f")
+        w_f = const.tile([P, G], F32, name="w_f")
         wh_bc = const.tile([P, G], BF16, name="wh_bc")
-        cw_bc = const.tile([P, H], BF16, name="cw_bc")
-        cb_bc = const.tile([P, H], BF16, name="cb_bc")
         g_hl = const.tile([P, 2, P + 2], BF16, name="g_hl")
         v_t = const.tile([P, 48], F32, name="v_t")
         b_t = const.tile([P, 16], F32, name="b_t")
@@ -119,27 +70,164 @@ def tile_multilstm_pa_t_kernel(
         var_a = const.tile([P, NT], F32, name="var_a")
         ve_a = const.tile([P, NT], F32, name="ve_a")
         rs_a = const.tile([P, NT], F32, name="rs_a")
-        nb_a = const.tile([P, NT], F32, name="nb_a")
+        x_sb = const.tile([P, NT, V], BF16, name="x_sb")
+        w_n = const.tile([P, 16, V], BF16, name="w_n")
+        w_s = const.tile([P, 16, V], F32, name="w_s")
+        vec = const.tile([P, P], BF16, name="vec")
+        nc.vector.memset(vec[:], 0.0)
+        rows_b = const.tile([P, G + 2 * H], BF16, name="rows_b")
+        nc.gpsimd.memset(rows_b[:], 0.0)
+        st_r = []
+        for i in range(3):
+            st = const.tile([P, 18], F32, name="st_r%d" % i)
+            nc.vector.memset(st[:], float(H))
+            st_r.append(st)
+        lnc_bank = psum.tile([P, 2, H], BF16, name="lnc_ps", tag="c", bufs=1)
 
-        s_bank, q_bank, st_r, a_bank, t_bank, p_bank = {}, {}, {}, {}, {}, {}
-        gt, so, mv_r, rs_r, ahat, p2t, c0s = {}, {}, {}, {}, {}, {}, {}
-        c1s, c2s, ys, cys, tcs, mv_c, rs_c = {}, {}, {}, {}, {}, {}, {}
-        nmu_c, var_c = {}, {}
+        r_bank, a_bank, y_bank = {}, {}, {}
+        gt, so, mv_r, rs_r, c0s = {}, {}, {}, {}, {}
+        c1s, c2s, cys, tcs, st_c, rs_c = {}, {}, {}, {}, {}, {}
+        raws, groupeds, xss = {}, {}, {}
 
         def inside(i):
             return 0 <= i < NT
 
-        def rsqrt_eps(var, tag, bufs):
-            ve = small.tile([P, 1], F32, name="ve_" + tag, tag="ve_" + tag)
-            nc.gpsimd.tensor_scalar(out=ve[:], in0=var, scalar1=EPS, scalar2=1.0, op0=ALU.add, op1=ALU.mult)
-            rs = small.tile([P, 1], F32, name="rs_" + tag, tag="rs_" + tag, bufs=bufs)
-            nc.gpsimd.tensor_tensor(out=rs[:], in0=ve[:], in1=mhalf[:, 0:1], op=ALU.pow)
-            return rs
+        def load_rows(j):
+            src = whh_v[:, ST * (j + 4):ST * (j + 5), :] if j < 0 else h0_v[:, ST * j:ST * (j + 1), :]
+            raws[j] = work.tile([P, ST * H], BF16, name="raw", tag="raw", bufs=5)
+            nc.sync.dma_start(out=raws[j][:].rearrange("p (t k) -> p t k", t=ST), in_=src)
 
-        def r_pass(t, c):
+        def pack_half(j, half, tag, bufs, eng):
+            words = raws[j][:].bitcast(F32)
+            if half == 0:
+                groupeds[j] = work.tile([P, ST * P * 4], BF16, name="grouped", tag="grouped", bufs=3, align_bytes=64)
+            g_words = groupeds[j][:].bitcast(F32).rearrange("p (t c u) -> p t c u", t=ST, u=2)
+            bank = psum.tile([P, 2, 2, P], F32, name="tp_w", tag=tag, bufs=bufs)
+            for i in range(2):
+                for u in range(2):
+                    first = (2 * half + i) * (H // 2)
+                    nc.tensor.transpose(bank[:, i, u, :], words[:, first + u:first + H // 2:2], ident_f[:])
+            dst, src = g_words[:, 2 * half:2 * half + 2, :, :], bank[:].rearrange("p t u c -> p t c u")
+            if eng == "v":
+                nc.vector.tensor_copy(out=dst, in_=src)
+            else:
+                nc.scalar.copy(out=dst, in_=src)
+
+        def quant(j):
+            first = (j + 4 if j < 0 else j) * H
+            cols = slice(first, first + H)
+            codes, scales = (w_codes[:, cols], w_scales[:, cols]) if j < 0 else (h_codes[:, cols], h_scales[:, cols])
+            nc.vector.quantize_mx(out=codes.bitcast(FP8X4), scales=scales, in_=groupeds[j][:])
+
+        def spread(dst, first):
+            bank = psum.tile([P, H], F32, name="b_ps", tag="a", bufs=3)
+            nc.tensor.matmul(bank[:], lhsT=ones_sq[:], rhs=rows_b[:, first:first + H], start=True, stop=True)
+            nc.scalar.copy(out=dst, in_=bank[:])
+
+        def spread_lnc():
+            for i in range(2):
+                nc.tensor.matmul(
+                    lnc_bank[:, i, :], lhsT=ones_sq[:], rhs=rows_b[:, G + i * H:G + (i + 1) * H], start=True, stop=True
+                )
+
+        def vec_t():
+            bank = psum.tile([P, P], BF16, name="tp_v", tag="a", bufs=3)
+            nc.tensor.transpose(bank[:], vec[:], ident_b[:])
+            nc.vector.tensor_copy(out=v_t[:], in_=bank[:, 0:48])
+            nc.vector.tensor_tensor(out=b_t[:], in0=v_t[:, 16:32], in1=v_t[:, 32:48], op=ALU.add)
+
+        def flip_x(g):
+            bank = psum.tile([P, 4, P], BF16, name="tp_b", tag="a", bufs=3)
+            for i in range(4):
+                nc.tensor.transpose(bank[:, i, :], x_sb[:, 4 * g + i, :], ident_b[:])
+            nc.scalar.copy(out=x_t[:, 4 * g * P:4 * (g + 1) * P], in_=bank[:].rearrange("p t c -> p (t c)"))
+
+        def flip_f(dst, src, g):
+            bank = psum.tile([P, 4, P], F32, name="tp_f", tag="a", bufs=3)
+            for i in range(4):
+                nc.tensor.transpose(bank[:, i, :], src[:, i, :], ident_f[:])
+            nc.scalar.copy(out=dst[:, 4 * g * P:4 * (g + 1) * P], in_=bank[:].rearrange("p t c -> p (t c)"))
+
+        def gram():
+            g_ps = psum.tile([P, P + 2], F32, name="g_ps", tag="a", bufs=3)
+            for t in range(16):
+                nc.tensor.matmul(g_ps[:, 0:P], lhsT=w_n[:, t, :], rhs=w_n[:, t, :], start=(t == 0), stop=(t == 15))
+            for t in range(16):
+                nc.tensor.matmul(g_ps[:, P:P + 2], lhsT=w_n[:, t, :], rhs=ones_b[:], start=(t == 0), stop=(t == 15))
+            nc.vector.tensor_copy(out=g_hl[:, 0, :], in_=g_ps[:])
+            nc.vector.tensor_tensor(out=g_hl[:, 1, :], in0=g_ps[:], in1=g_hl[:, 0, :], op=ALU.subtract)
+
+        def center():
+            bank = psum.tile([P, V], F32, name="m_ps", tag="a", bufs=3)
+            for t in range(16):
+                nc.tensor.matmul(bank[:], lhsT=ones_sq[:], rhs=w_n[:, t, :], start=(t == 0), stop=(t == 15))
+            nc.vector.scalar_tensor_tensor(
+                out=w_s[:],
+                in0=bank[:].unsqueeze(1).to_broadcast([P, 16, V]),
+                scalar=-1.0 / G,
+                in1=w_n[:],
+                op0=ALU.mult,
+                op1=ALU.add,
+            )
+
+        def gain():
+            for t in range(16):
+                nc.gpsimd.tensor_scalar(
+                    out=w_s[:, t, :], in0=w_s[:, t, :], scalar1=v_t[:, t:t + 1], scalar2=0.0, op0=ALU.mult, op1=ALU.add
+                )
+
+        def a_mm(t0):
+            y_ps = psum.tile([P, 2, P + 2], F32, name="y_ps", tag="a", bufs=3)
+            for i in range(2):
+                lhs = x_t[:, (t0 + i) * P:(t0 + i + 1) * P]
+                nc.tensor.matmul(y_ps[:, i, :], lhsT=lhs, rhs=g_hl[:, 0, :], start=True, stop=False)
+                nc.tensor.matmul(y_ps[:, i, :], lhsT=lhs, rhs=g_hl[:, 1, :], start=False, stop=True)
+            y_bank[t0] = y_ps
+
+        def a_red(t0):
+            y_ps = y_bank[t0]
+            for i in range(2):
+                junk = small.tile([P, P], F32, name="junk", tag="junk")
+                nc.vector.scalar_tensor_tensor(
+                    out=junk[:],
+                    in0=y_ps[:, i, 0:P],
+                    scalar=1.0,
+                    in1=x_sb[:, t0 + i, :],
+                    op0=ALU.mult,
+                    op1=ALU.mult,
+                    accum_out=sumsq_a[:, t0 + i:t0 + i + 1],
+                )
+            nc.vector.tensor_copy(out=sum_a[:, t0:t0 + 2], in_=y_ps[:, :, P])
+
+        def a_stat(g):
+            for t0 in (4 * g, 4 * g + 2):
+                a_mm(t0)
+                a_red(t0)
+
+        def a_finish(lo, hi):
+            c = slice(lo, hi)
+            nc.vector.tensor_scalar(out=mu_a[:, c], in0=sum_a[:, c], scalar1=1.0 / G, scalar2=None, op0=ALU.mult)
+            nc.vector.tensor_tensor(out=musq_a[:, c], in0=mu_a[:, c], in1=mu_a[:, c], op=ALU.mult)
+            nc.vector.scalar_tensor_tensor(
+                out=var_a[:, c], in0=sumsq_a[:, c], scalar=1.0 / G, in1=musq_a[:, c], op0=ALU.mult, op1=ALU.subtract
+            )
+            nc.vector.tensor_scalar(out=ve_a[:, c], in0=var_a[:, c], scalar1=0.0, scalar2=EPS, op0=ALU.max, op1=ALU.add)
+            nc.gpsimd.tensor_tensor(out=rs_a[:, c], in0=ve_a[:, c], in1=mhalf[:, c], op=ALU.pow)
+
+        def x_scale(g):
+            xss[g] = small.tile([P, 4, V], F32, name="xs", tag="xs")
+            for i in range(4):
+                t = 4 * g + i
+                nc.gpsimd.tensor_scalar(
+                    out=xss[g][:, i, :], in0=x_sb[:, t, :], scalar1=rs_a[:, t:t + 1], scalar2=0.0, op0=ALU.mult, op1=ALU.add
+                )
+
+        def fill_r(t, c):
+            if not inside(t):
+                return
             rows = slice(t * P, (t + 1) * P)
             cols = slice(c * H, (c + 1) * H)
-            bank = psum.tile([P, H], F32, name="r_ps", tag="vs", bufs=4)
+            bank = psum.tile([P, H], F32, name="r_ps", tag="r", bufs=4)
             nc.tensor.matmul_mx(
                 out=bank[:],
                 lhsT=h_codes[:, rows].bitcast(FP8X4),
@@ -149,395 +237,284 @@ def tile_multilstm_pa_t_kernel(
                 start=True,
                 stop=True,
             )
-            return bank
+            r_bank[(t, c)] = bank
 
-        def fill_st(t, c):
+        def stat_v(t, c):
             if inside(t):
-                s_bank[(t, c)] = r_pass(t, c)
+                nc.vector.bn_stats(out=st_r[t % 3][:, 6 * c:6 * c + 6], in_=r_bank[(t, c)][:])
 
-        def fill_q(t, c):
+        def junk_b():
+            return small.tile([P, H], BF16, name="junk_b", tag="junk_b")
+
+        def stat_mean(t, c):
             if inside(t):
-                q_bank[(t, c)] = r_pass(t, c)
+                col = 12 + 3 * (c - 2)
+                nc.scalar.activation(
+                    out=junk_b()[:], in_=r_bank[(t, c)][:], func=ACT.Identity, scale=1.0 / H,
+                    accum_out=st_r[t % 3][:, col + 1:col + 2],
+                )
 
-        def rd_st(t, c):
-            if not inside(t):
-                return
-            if c == 0:
-                st_r[t] = small.tile([P, 4, 6], F32, name="st_r", tag="st_r")
-            nc.vector.bn_stats(out=st_r[t][:, c, :], in_=s_bank[(t, c)][:])
+        def stat_dev(t, c):
+            if inside(t):
+                col = 12 + 3 * (c - 2)
+                st = st_r[t % 3]
+                nc.scalar.activation(
+                    out=junk_b()[:], in_=r_bank[(t, c)][:], func=ACT.Square, scale=-1.0,
+                    bias=st[:, col + 1:col + 2], accum_out=st[:, col + 2:col + 3],
+                )
 
         def aggr(t):
-            if not inside(t):
-                return
-            mv = small.tile([P, 2], F32, name="mv_r", tag="mv_r", bufs=3)
-            nc.vector.bn_aggr(out=mv[:], in_=st_r[t][:].rearrange("p c s -> p (c s)"))
-            mv_r[t] = mv
-            rs_r[t] = rsqrt_eps(mv[:, 1:2], "r", 11)
+            if inside(t):
+                mv_r[t] = small.tile([P, 2], F32, name="mv_r", tag="mv_r", bufs=3)
+                nc.vector.bn_aggr(out=mv_r[t][:], in_=st_r[t % 3][:])
 
-        def rd_q(t, c):
+        def rsqrt(t_r, t_c):
+            ve = small.tile([P, 2], F32, name="ve", tag="ve")
+            rs = small.tile([P, 2], F32, name="rs", tag="rs", bufs=LEAD + 3)
+            if inside(t_r):
+                nc.gpsimd.tensor_scalar(
+                    out=ve[:, 0:1], in0=mv_r[t_r][:, 1:2], scalar1=1.0, scalar2=EPS, op0=ALU.mult, op1=ALU.add
+                )
+                rs_r[t_r] = rs[:, 0:1]
+            if inside(t_c):
+                nc.gpsimd.tensor_scalar(
+                    out=ve[:, 1:2], in0=st_c[t_c][:, 1:2], scalar1=1.0 / H, scalar2=EPS, op0=ALU.mult, op1=ALU.add
+                )
+                rs_c[t_c] = rs[:, 1:2]
+            cols = slice(0 if inside(t_r) else 1, 2 if inside(t_c) else 1)
+            if inside(t_r) or inside(t_c):
+                nc.gpsimd.tensor_tensor(out=rs[:, cols], in0=ve[:, cols], in1=mhalf[:, cols], op=ALU.pow)
+
+        def scale_r(t, c):
             if not inside(t):
                 return
-            if c == 0:
-                gt[t] = gates.tile([P, G], F32, name="gate", tag="gate")
+            if t not in gt:
+                gt[t] = work.tile([P, G], F32, name="gate", tag="gate", bufs=LEAD + 4)
             cols = slice(c * H, (c + 1) * H)
             nc.vector.scalar_tensor_tensor(
-                out=gt[t][:, cols],
-                in0=q_bank[(t, c)][:],
-                scalar=mv_r[t][:, 0:1],
-                in1=wh_bc[:, cols],
-                op0=ALU.subtract,
-                op1=ALU.mult,
+                out=gt[t][:, cols], in0=r_bank[(t, c)][:], scalar=mv_r[t][:, 0:1], in1=wh_bc[:, cols],
+                op0=ALU.subtract, op1=ALU.mult,
             )
 
-        def am(k, bt):
-            if not inside(k):
+        def fill_a(t, c):
+            if not inside(t):
                 return
-            s, c = divmod(k, 4)
-            t = ST * s + bt
-            bank = psum.tile([P, H], F32, name="a_ps", tag="ss", bufs=4)
+            bank = psum.tile([P, H], F32, name="a_ps", tag="a", bufs=3)
             nc.tensor.matmul(
-                bank[:], lhsT=x_t[:, t * P:(t + 1) * P], rhs=w_t[:, c * H:(c + 1) * H], start=True, stop=True
+                bank[:], lhsT=x_f[:, t * P:(t + 1) * P], rhs=w_f[:, c * H:(c + 1) * H], start=True, stop=False
             )
-            a_bank[(k, bt)] = bank
-
-        def ah(k, bt):
-            if not inside(k):
-                return
-            t = ST * (k // 4) + bt
-            if bt == 0:
-                ahat[k] = work.tile([P, ST, H], F32, name="ahat", tag="ahat")
-            nc.scalar.activation(
-                out=ahat[k][:, bt, :],
-                in_=a_bank[(k, bt)][:],
-                func=ACT.Identity,
-                bias=nb_a[:, t:t + 1],
-                scale=rs_a[:, t:t + 1],
-            )
-
-        def tb(k, jb):
-            if not inside(k):
-                return
-            bank = psum.tile([P, ST, P], F32, name="t_ps", tag="ss", bufs=4)
-            for bt in range(ST):
-                nc.tensor.transpose(bank[:, bt, :], ahat[k][:, bt, jb * P:(jb + 1) * P], ident_f[:])
-            t_bank[(k, jb)] = bank
-
-        def pt(k, jb):
-            if not inside(k):
-                return
-            if jb == 0:
-                p2t[k] = work.tile([P, 4, ST * P], F32, name="p2t", tag="p2t")
-            col = 4 * (k % 4) + jb
-            nc.scalar.activation(
-                out=p2t[k][:, jb, :],
-                in_=t_bank[(k, jb)][:].rearrange("p t b -> p (t b)"),
-                func=ACT.Identity,
-                bias=b_t[:, col:col + 1],
-                scale=v_t[:, col:col + 1],
-            )
-
-        def p2(k, bt):
-            if not inside(k):
-                return
-            bank = psum.tile([P, 4, P], F32, name="p_ps", tag="vs", bufs=4)
             for jb in range(4):
-                nc.tensor.transpose(bank[:, jb, :], p2t[k][:, jb, bt * P:(bt + 1) * P], ident_f[:])
-            p_bank[(k, bt)] = bank
+                col = 4 * c + jb
+                nc.tensor.matmul(
+                    bank[:, jb * P:(jb + 1) * P],
+                    lhsT=b_t[:, col:col + 1].to_broadcast([P, P]),
+                    rhs=ident_f[:],
+                    is_transpose=True,
+                    start=False,
+                    stop=(jb == 3),
+                )
+            a_bank[(t, c)] = bank
 
-        def z(k, bt):
-            if not inside(k):
-                return
-            s, c = divmod(k, 4)
-            t = ST * s + bt
-            dst = gt[t][:, c * H:(c + 1) * H]
-            nc.vector.scalar_tensor_tensor(
-                out=dst,
-                in0=dst,
-                scalar=rs_r[t][:, 0:1],
-                in1=p_bank[(k, bt)][:].rearrange("p j c -> p (j c)"),
-                op0=ALU.mult,
-                op1=ALU.add,
-            )
+        def z(t, c):
+            if inside(t):
+                dst = gt[t][:, c * H:(c + 1) * H]
+                nc.vector.scalar_tensor_tensor(
+                    out=dst, in0=dst, scalar=rs_r[t], in1=a_bank[(t, c)][:], op0=ALU.mult, op1=ALU.add
+                )
 
-        def act(k, bt):
-            if not inside(k):
+        def act(t, c):
+            if not inside(t):
                 return
-            s, c = divmod(k, 4)
-            t = ST * s + bt
             src = gt[t][:, c * H:(c + 1) * H]
             if c == 3:
-                so[t] = cellp[0].tile([P, H], F32, name="so", tag="so", bufs=8)
+                so[t] = work.tile([P, H], F32, name="so", tag="so", bufs=4)
                 nc.scalar.activation(out=so[t][:], in_=src, func=ACT.Sigmoid)
             else:
                 nc.scalar.activation(out=src, in_=src, func=(ACT.Tanh if c == 2 else ACT.Sigmoid))
 
         def c1op(t, eng):
-            s, bt = divmod(t, ST)
-            c1s[t] = cellp[0].tile([P, H], F32, name="c1", tag="c1", bufs=C1_BUFS)
-            eng.tensor_tensor(out=c1s[t][:], in0=gt[t][:, H:2 * H], in1=c0s[s][:, bt, :], op=ALU.mult)
+            if inside(t):
+                s, bt = divmod(t, ST)
+                c1s[t] = work.tile([P, H], F32, name="c1", tag="c1", bufs=4)
+                eng.tensor_tensor(out=c1s[t][:], in0=gt[t][:, H:2 * H], in1=c0s[s][:, bt, :], op=ALU.mult)
 
         def c2op(t, eng):
-            c2s[t] = cellp[0].tile([P, H], F32, name="c2", tag="c2", bufs=C2_BUFS)
-            eng.tensor_tensor(out=c2s[t][:], in0=gt[t][:, 0:H], in1=gt[t][:, 2 * H:3 * H], op=ALU.mult)
+            if inside(t):
+                c2s[t] = work.tile([P, H], F32, name="c2", tag="c2")
+                eng.tensor_tensor(out=c2s[t][:], in0=gt[t][:, 0:H], in1=gt[t][:, 2 * H:3 * H], op=ALU.mult)
 
         def csum(t, eng):
-            eng.tensor_tensor(out=c1s[t][:], in0=c1s[t][:], in1=c2s[t][:], op=ALU.add)
+            if inside(t):
+                eng.tensor_tensor(out=c1s[t][:], in0=c1s[t][:], in1=c2s[t][:], op=ALU.add)
 
-        def cstat(t):
-            if not inside(t):
-                return
-            st6 = small.tile([P, 6], F32, name="st_c", tag="st_c")
-            nc.vector.bn_stats(out=st6[:], in_=c1s[t][:])
-            mv = small.tile([P, 2], F32, name="mv_c", tag="mv_c", bufs=3)
-            nc.vector.bn_aggr(out=mv[:], in_=st6[:])
-            mv_c[t] = mv
+        def cell_mean(t):
+            if inside(t):
+                st_c[t] = small.tile([P, 2], F32, name="st_c", tag="st_c", bufs=3)
+                nc.scalar.activation(
+                    out=junk_b()[:], in_=c1s[t][:], func=ACT.Identity, scale=1.0 / H, accum_out=st_c[t][:, 0:1]
+                )
 
-        def cs1(t):
-            junk = small.tile([P, H], BF16, name="junk_c", tag="junk_c")
-            total = small.tile([P, 1], F32, name="sum_c", tag="sum_c")
-            nc.scalar.activation(out=junk[:], in_=c1s[t][:], func=ACT.Identity, accum_out=total[:])
-            nmu_c[t] = small.tile([P, 1], F32, name="nmu_c", tag="nmu_c", bufs=3)
-            nc.scalar.activation(out=nmu_c[t][:], in_=total[:], func=ACT.Identity, scale=-1.0 / H)
-
-        def cs2(t):
-            junk = small.tile([P, H], BF16, name="junk_c", tag="junk_c")
-            ssq = small.tile([P, 1], F32, name="ssq_c", tag="ssq_c")
-            nc.scalar.activation(out=junk[:], in_=c1s[t][:], func=ACT.Square, bias=nmu_c[t][:, 0:1], accum_out=ssq[:])
-            var_c[t] = small.tile([P, 1], F32, name="var_c", tag="var_c", bufs=3)
-            nc.scalar.activation(out=var_c[t][:], in_=ssq[:], func=ACT.Identity, scale=1.0 / H)
-
-        def cpow(t):
-            if not inside(t):
-                return
-            rs_c[t] = rsqrt_eps(var_c[t][:, 0:1] if t in var_c else mv_c[t][:, 1:2], "c", 3)
+        def cell_dev(t):
+            if inside(t):
+                nc.scalar.activation(
+                    out=junk_b()[:], in_=c1s[t][:], func=ACT.Square, scale=-1.0, bias=st_c[t][:, 0:1],
+                    accum_out=st_c[t][:, 1:2],
+                )
 
         def yop(t):
-            if not inside(t):
-                return
-            ys[t] = cellp[0].tile([P, H], F32, name="y", tag="y")
-            nc.vector.scalar_tensor_tensor(
-                out=ys[t][:],
-                in0=c1s[t][:],
-                scalar=(nmu_c[t][:, 0:1] if t in nmu_c else mv_c[t][:, 0:1]),
-                in1=cw_bc[:],
-                op0=(ALU.add if t in nmu_c else ALU.subtract),
-                op1=ALU.mult,
-            )
+            if inside(t):
+                nc.vector.scalar_tensor_tensor(
+                    out=c1s[t][:], in0=c1s[t][:], scalar=st_c[t][:, 0:1], in1=lnc_bank[:, 0, :],
+                    op0=ALU.subtract, op1=ALU.mult,
+                )
 
         def cyop(t):
-            if not inside(t):
-                return
-            cys[t] = cellp[0].tile([P, H], F32, name="cy", tag="cy", bufs=3)
-            nc.vector.scalar_tensor_tensor(
-                out=cys[t][:], in0=ys[t][:], scalar=rs_c[t][:, 0:1], in1=cb_bc[:], op0=ALU.mult, op1=ALU.add
-            )
-            nc.sync.dma_start(out=cy_v[:, t, :], in_=cys[t][:])
+            if inside(t):
+                cys[t] = work.tile([P, H], F32, name="cy", tag="cy", bufs=3)
+                nc.vector.scalar_tensor_tensor(
+                    out=cys[t][:], in0=c1s[t][:], scalar=rs_c[t], in1=lnc_bank[:, 1, :],
+                    op0=ALU.mult, op1=ALU.add,
+                )
+
+        def store_cy(t):
+            if inside(t):
+                nc.sync.dma_start(out=cy_v[:, t, :], in_=cys[t][:])
 
         def th(t):
-            if not inside(t):
-                return
-            tcs[t] = cellp[0].tile([P, H], F32, name="tcy", tag="tcy", bufs=3)
-            nc.scalar.activation(out=tcs[t][:], in_=cys[t][:], func=ACT.Tanh)
+            if inside(t):
+                tcs[t] = work.tile([P, H], F32, name="tcy", tag="tcy")
+                nc.scalar.activation(out=tcs[t][:], in_=cys[t][:], func=ACT.Tanh)
 
         def hyop(t, eng):
-            hy = cellp[0].tile([P, H], F32, name="hy", tag="hy", bufs=4)
-            eng.tensor_tensor(out=hy[:], in0=so[t][:], in1=tcs[t][:], op=ALU.mult)
-            nc.sync.dma_start(out=hy_v[:, t, :], in_=hy[:])
+            if inside(t):
+                hy = work.tile([P, H], F32, name="hy", tag="hy")
+                eng.tensor_tensor(out=hy[:], in0=so[t][:], in1=tcs[t][:], op=ALU.mult)
+                nc.sync.dma_start(out=hy_v[:, t, :], in_=hy[:])
 
+        def load_c0(s):
+            if 0 <= s < NT // ST:
+                c0s[s] = work.tile([P, ST, H], BF16, name="c0_sb", tag="c0_sb", bufs=2)
+                nc.sync.dma_start(out=c0s[s][:], in_=c0_v[:, ST * s:ST * (s + 1), :])
 
-        two_input = {"c1": c1op, "c2": c2op, "csum": csum, "hy": hyop}
-        one_engine = {"cstat": cstat, "cpow": cpow, "y": yop, "cy": cyop, "th": th, "cs1": cs1, "cs2": cs2}
-        plan = CELL_PLAN()
+        prep = {}
 
-        def slot(n, prep):
-            if n % ST == 0 and inside(n):
-                c0s[n // ST] = work.tile([P, ST, H], BF16, name="c0_sb", tag="c0_sb", bufs=3)
-                nc.sync.dma_start(out=c0s[n // ST][:], in_=c0_v[:, n:n + ST, :])
-            for i in range(4):
-                n1, i1 = divmod(4 * n + i + 1, 4)
-                n2, i2 = divmod(4 * n + i + 2, 4)
-                ah(n + 2, i)
-                tb(n1 + 1, i1)
-                pt(n + 1, i)
-                am(n2 + 2, i2)
-                act(n - 1, i)
-                fill_st(n1 + 5, i1)
-                rd_st(n + 5, i)
-                fill_q(n1 + 4, i1)
-                rd_q(n + 4, i)
-                p2(n1, i1)
-                z(n, i)
-                for name, t, on_vector in plan.get((n, i), []):
-                    if name in two_input:
-                        two_input[name](t, nc.vector if on_vector else nc.gpsimd)
-                    else:
-                        one_engine[name](t)
-                if i == 3:
-                    aggr(n + 5)
-                for job in prep.get((n, i), []):
-                    job()
+        def put(n, q, job, *args):
+            prep.setdefault((n, q), []).append((job, args))
 
-        with tc.tile_pool(name="pro", bufs=1) as pro, tc.tile_pool(name="stage", bufs=2) as stg:
-            x_sb = pro.tile([P, NT, V], BF16, name="x_sb")
-            w_n = pro.tile([P, 16, V], BF16, name="w_n")
-            vec = pro.tile([P, P], BF16, name="vec")
-            nc.vector.memset(vec[:], 0.0)
+        first = -LEAD - 1
+        put(first, 0, lambda: flip_f(w_f, w_s[:, 4:8, :], 1))
+        put(first, 1, lambda: flip_f(w_f, w_s[:, 0:4, :], 0))
+        put(first, 2, lambda: flip_f(x_f, xss[0][:], 0))
+        put(first, 3, lambda: flip_f(w_f, w_s[:, 8:12, :], 2))
+        put(first + 1, 0, lambda: flip_f(w_f, w_s[:, 12:16, :], 3))
+        put(first + 1, 1, spread_lnc)
+        put(first, 3, pack_half, 1, 0, "a", 3, "s")
+        put(first + 1, 2, pack_half, 1, 1, "a", 3, "s")
+        put(first + 1, 3, quant, 1)
+        for g in range(1, 8):
+            n = ST * (g - 2)
+            put(g - 2, 3, x_scale, g)
+            put(g - 1, 0, lambda g: flip_f(x_f, xss[g][:], g), g)
+            if g > 1:
+                put(n + 1, 0, pack_half, g, 0, "a", 3, "s")
+                put(n + 2, 0, pack_half, g, 1, "a", 3, "s")
+                put(n + 3, 2, quant, g)
+            if g + 1 < 8:
+                put(max(n + 2, first), 1, load_rows, g + 1)
+            put(max(n + 4, first), 2, load_c0, g)
 
-            raws = {}
-            groupeds = {}
-            y_bank = {}
-
-            def load_rows(j):
-                if 1 <= j <= 4:
-                    src = whh_v[:, ST * (j - 1):ST * j, :]
+        def slot(n):
+            for q in range(4):
+                t_z, q_z = divmod(4 * n + q - 1, 4)
+                t_a, q_a = divmod(4 * n + q + 2, 4)
+                if q == 0:
+                    scale_r(n + LEAD, 2)
+                    scale_r(n + LEAD, 3)
+                    act(t_z, CHUNK_ORDER[q_z])
+                    cell_dev(n - 2)
+                    hyop(n - 3, nc.gpsimd)
+                    rsqrt(n + LEAD, n - 2)
+                elif q == 1:
+                    fill_r(n + LEAD + 1, 2)
+                    fill_r(n + LEAD + 1, 3)
+                    scale_r(n + LEAD, 0)
+                    scale_r(n + LEAD, 1)
+                    act(t_z, CHUNK_ORDER[q_z])
+                    stat_mean(n + LEAD + 1, 2)
+                    stat_mean(n + LEAD + 1, 3)
+                    c2op(n - 1, nc.gpsimd)
+                elif q == 2:
+                    fill_r(n + LEAD + 1, 0)
+                    fill_r(n + LEAD + 1, 1)
+                    yop(n - 2)
+                    act(t_z, CHUNK_ORDER[q_z])
+                    stat_dev(n + LEAD + 1, 2)
+                    stat_dev(n + LEAD + 1, 3)
+                    csum(n - 1, nc.gpsimd)
                 else:
-                    s = max(j - 4, 0)
-                    src = h0_v[:, ST * s:ST * (s + 1), :]
-                raws[j] = stg.tile([P, ST * H], BF16, name="raw", tag="raw", bufs=RAW_BUFS)
-                nc.sync.dma_start(out=raws[j][:].rearrange("p (t k) -> p t k", t=ST), in_=src)
+                    stat_v(n + LEAD + 1, 0)
+                    stat_v(n + LEAD + 1, 1)
+                    act(t_z, CHUNK_ORDER[q_z])
+                    cell_mean(n - 1)
+                    th(n - 2)
+                    c1op(n, nc.gpsimd)
+                fill_a(t_a, CHUNK_ORDER[q_a])
+                z(n, CHUNK_ORDER[q])
+                if q == 2:
+                    cyop(n - 2)
+                    store_cy(n - 2)
+                if q == 3:
+                    aggr(n + LEAD + 1)
+                for job, args in prep.get((n, q), []):
+                    job(*args)
 
-            def pack_rows(j):
-                words = raws[j][:].bitcast(F32)
-                grouped = stg.tile([P, ST * P * 4], BF16, name="grouped", tag="grouped", bufs=GROUPED_BUFS, align_bytes=64)
-                groupeds[j] = grouped
-                g_words = grouped[:].bitcast(F32).rearrange("p (t c u) -> p t c u", t=ST, u=2)
-                for half in range(2):
-                    bank = psum.tile([P, 2, 2, P], F32, name="tp_w", tag="ss")
-                    for i in range(2):
-                        for u in range(2):
-                            first = (2 * half + i) * (H // 2)
-                            nc.tensor.transpose(bank[:, i, u, :], words[:, first + u:first + H // 2:2], ident_f[:])
-                    nc.scalar.copy(
-                        out=g_words[:, 2 * half:2 * half + 2, :, :], in_=bank[:].rearrange("p t u c -> p t c u")
-                    )
-                if j + RAW_BUFS < 12:
-                    load_rows(j + RAW_BUFS)
-
-            def quant_rows(j):
-                is_w = 1 <= j <= 4
-                first = (j - 1 if is_w else max(j - 4, 0)) * H
-                cols = slice(first, first + H)
-                codes = w_codes[:, cols] if is_w else h_codes[:, cols]
-                scales = w_scales[:, cols] if is_w else h_scales[:, cols]
-                nc.vector.quantize_mx(out=codes.bitcast(FP8X4), scales=scales, in_=groupeds[j][:])
-
-            def vec_t():
-                bank = psum.tile([P, P], BF16, name="tp_v", tag="vs")
-                nc.tensor.transpose(bank[:], vec[:], ident_b[:])
-                nc.vector.tensor_copy(out=v_t[:], in_=bank[:, 0:48])
-                nc.vector.tensor_tensor(out=b_t[:], in0=v_t[:, 16:32], in1=v_t[:, 32:48], op=ALU.add)
-
-            def flip(dst, src, g):
-                bank = psum.tile([P, 4, P], BF16, name="tp_b", tag="ss")
-                for i in range(4):
-                    nc.tensor.transpose(bank[:, i, :], src[:, 4 * g + i, :], ident_b[:])
-                nc.scalar.copy(out=dst[:, 4 * g * P:4 * (g + 1) * P], in_=bank[:].rearrange("p t c -> p (t c)"))
-
-            def gram():
-                g_ps = psum.tile([P, P + 2], F32, name="g_ps", tag="vs")
-                for t in range(16):
-                    nc.tensor.matmul(
-                        g_ps[:, 0:P], lhsT=w_n[:, t, :], rhs=w_n[:, t, :], start=(t == 0), stop=(t == 15)
-                    )
-                for t in range(16):
-                    nc.tensor.matmul(
-                        g_ps[:, P:P + 2], lhsT=w_n[:, t, :], rhs=ones_b[:], start=(t == 0), stop=(t == 15)
-                    )
-                nc.vector.tensor_copy(out=g_hl[:, 0, :], in_=g_ps[:])
-                nc.vector.tensor_tensor(out=g_hl[:, 1, :], in0=g_ps[:], in1=g_hl[:, 0, :], op=ALU.subtract)
-
-            def a_mm(t0):
-                y_ps = psum.tile([P, 2, P + 2], F32, name="y_ps", tag="ss")
-                for i in range(2):
-                    lhs = x_t[:, (t0 + i) * P:(t0 + i + 1) * P]
-                    nc.tensor.matmul(y_ps[:, i, :], lhsT=lhs, rhs=g_hl[:, 0, :], start=True, stop=False)
-                    nc.tensor.matmul(y_ps[:, i, :], lhsT=lhs, rhs=g_hl[:, 1, :], start=False, stop=True)
-                y_bank[t0] = y_ps
-
-            def a_red(t0):
-                y_ps = y_bank[t0]
-                for i in range(2):
-                    junk = pro.tile([P, P], F32, name="junk", tag="junk", bufs=2)
-                    nc.vector.scalar_tensor_tensor(
-                        out=junk[:],
-                        in0=y_ps[:, i, 0:P],
-                        scalar=1.0,
-                        in1=x_sb[:, t0 + i, :],
-                        op0=ALU.mult,
-                        op1=ALU.mult,
-                        accum_out=sumsq_a[:, t0 + i:t0 + i + 1],
-                    )
-                nc.vector.tensor_copy(out=sum_a[:, t0:t0 + 2], in_=y_ps[:, :, P])
-
-            def a_finish(lo, hi):
-                c = slice(lo, hi)
-                nc.vector.tensor_scalar(out=mu_a[:, c], in0=sum_a[:, c], scalar1=1.0 / G, scalar2=None, op0=ALU.mult)
-                nc.vector.tensor_tensor(out=musq_a[:, c], in0=mu_a[:, c], in1=mu_a[:, c], op=ALU.mult)
-                nc.vector.scalar_tensor_tensor(
-                    out=var_a[:, c], in0=sumsq_a[:, c], scalar=1.0 / G, in1=musq_a[:, c], op0=ALU.mult, op1=ALU.subtract
-                )
-                nc.vector.tensor_scalar(
-                    out=ve_a[:, c], in0=var_a[:, c], scalar1=0.0, scalar2=EPS, op0=ALU.max, op1=ALU.add
-                )
-                nc.gpsimd.tensor_tensor(out=rs_a[:, c], in0=ve_a[:, c], in1=mhalf[:, c], op=ALU.pow)
-
-            def a_bias(lo, hi):
-                c = slice(lo, hi)
-                nc.vector.scalar_tensor_tensor(
-                    out=nb_a[:, c], in0=mu_a[:, c], scalar=-1.0, in1=rs_a[:, c], op0=ALU.mult, op1=ALU.mult
-                )
-
-            rows_b = pro.tile([P, G + 2 * H], BF16, name="rows_b")
-            nc.vector.memset(rows_b[:], 0.0)
-            ones_sq = pro.tile([P, P], BF16, name="ones_sq")
-            nc.vector.memset(ones_sq[:], 1.0)
-
-            def spread(dst, first):
-                bank = psum.tile([P, H], F32, name="b_ps", tag="ss")
-                nc.tensor.matmul(bank[:], lhsT=ones_sq[:], rhs=rows_b[:, first:first + H], start=True, stop=True)
-                nc.scalar.copy(out=dst, in_=bank[:])
-
-            for j in range(RAW_BUFS):
+        with tc.manual_schedule():
+            nc.sync.dma_start(out=w_n[:], in_=wih_v)
+            for i in range(2):
+                nc.sync.dma_start(out=x_sb[:, 16 * i:16 * (i + 1), :], in_=x_v[:, 16 * i:16 * (i + 1), :])
+            load_rows(0)
+            load_rows(-2)
+            nc.sync.dma_start(out=vec[0:16, :], in_=lni_w1.rearrange("(t p) -> t p", p=P))
+            nc.sync.dma_start(out=vec[16:32, :], in_=lni_b1.rearrange("(t p) -> t p", p=P))
+            nc.sync.dma_start(out=vec[32:48, :], in_=lnh_b1.rearrange("(t p) -> t p", p=P))
+            for j in (-1, -4, -3):
                 load_rows(j)
             nc.sync.dma_start(out=rows_b[0:1, 0:G], in_=lnh_w1.rearrange("(o g) -> o g", o=1))
             nc.sync.dma_start(out=rows_b[0:1, G:G + H], in_=lnc_w1.rearrange("(o g) -> o g", o=1))
             nc.sync.dma_start(out=rows_b[0:1, G + H:G + 2 * H], in_=lnc_b1.rearrange("(o g) -> o g", o=1))
-            nc.sync.dma_start(out=w_n[:], in_=wih_v)
-            nc.sync.dma_start(out=x_sb[:], in_=x_v)
-            for j in range(5):
-                pack_rows(j)
-                quant_rows(j)
-            for c in range(4):
-                spread(wh_bc[:, c * H:(c + 1) * H], c * H)
-            nc.sync.dma_start(out=vec[0:16, :], in_=lni_w1.rearrange("(t p) -> t p", p=P))
-            nc.sync.dma_start(out=vec[16:32, :], in_=lni_b1.rearrange("(t p) -> t p", p=P))
-            nc.sync.dma_start(out=vec[32:48, :], in_=lnh_b1.rearrange("(t p) -> t p", p=P))
-            flip(w_t, w_n, 0)
-            flip(x_t, x_sb, 0)
+            load_rows(1)
+            load_c0(0)
+
+            def pack(j):
+                pack_half(j, 0, "r", 4, "s")
+                pack_half(j, 1, "r", 4, "v")
+                quant(j)
+
             gram()
-            for t0 in (0, 2):
-                a_mm(t0)
-                a_red(t0)
+            center()
+            for g in range(4):
+                flip_x(g)
+                a_stat(g)
             a_finish(0, 4)
-            a_bias(0, 4)
+            pack(0)
+            pack(-2)
             vec_t()
-            pack_rows(5)
-            quant_rows(5)
-            for g in range(1, 4):
-                flip(w_t, w_n, g)
-            for g in range(1, 8):
-                flip(x_t, x_sb, g)
-                for t0 in (4 * g, 4 * g + 2):
-                    a_mm(t0)
-                    a_red(t0)
-            a_finish(4, NT)
-            a_bias(4, NT)
-            spread(cw_bc[:], G)
-            spread(cb_bc[:], G + H)
-            for j in range(6, 12):
-                pack_rows(j)
-                quant_rows(j)
-        cellp.append(ctx.enter_context(tc.tile_pool(name="cellp", bufs=2)))
-        with tc.manual_schedule():
-            for n in range(-6, LAST_SLOT + 1):
-                slot(n, {})
+            gain()
+            x_scale(0)
+            flip_x(4)
+            a_stat(4)
+            pack(-1)
+            flip_x(5)
+            a_stat(5)
+            pack(-4)
+            flip_x(6)
+            a_stat(6)
+            pack(-3)
+            for c in (2, 3, 0, 1):
+                spread(wh_bc[:, c * H:(c + 1) * H], c * H)
+            flip_x(7)
+            a_stat(7)
+            a_finish(4, 16)
+            a_finish(16, NT)
+            for n in range(first, NT + DEPTH):
+                slot(n)

@@ -20,7 +20,6 @@ EPS = 1e-5
 FLOPS = 2 * B * G * (H + V)
 CHUNK_ORDER = (1, 0, 2, 3)
 LEAD = 1
-DEPTH = 3
 
 
 def tile_multilstm_pa_t_kernel(
@@ -83,6 +82,7 @@ def tile_multilstm_pa_t_kernel(
             nc.vector.memset(st[:], float(H))
             st_r.append(st)
         lnc_bank = psum.tile([P, 2, H], BF16, name="lnc_ps", tag="c", bufs=1)
+        warm = const.tile([P, 1], F32, name="warm")
 
         r_bank, a_bank, y_bank = {}, {}, {}
         gt, so, mv_r, rs_r, c0s = {}, {}, {}, {}, {}
@@ -91,6 +91,12 @@ def tile_multilstm_pa_t_kernel(
 
         def inside(i):
             return 0 <= i < NT
+
+        def copy_out(eng, dst, src):
+            if eng == "v":
+                nc.vector.tensor_copy(out=dst, in_=src)
+            else:
+                nc.scalar.copy(out=dst, in_=src)
 
         def load_rows(j):
             src = whh_v[:, ST * (j + 4):ST * (j + 5), :] if j < 0 else h0_v[:, ST * j:ST * (j + 1), :]
@@ -108,10 +114,7 @@ def tile_multilstm_pa_t_kernel(
                     first = (2 * half + i) * (H // 2)
                     nc.tensor.transpose(bank[:, i, u, :], words[:, first + u:first + H // 2:2], ident_f[:])
             dst, src = g_words[:, 2 * half:2 * half + 2, :, :], bank[:].rearrange("p t u c -> p t c u")
-            if eng == "v":
-                nc.vector.tensor_copy(out=dst, in_=src)
-            else:
-                nc.scalar.copy(out=dst, in_=src)
+            copy_out(eng, dst, src)
 
         def quant(j):
             first = (j + 4 if j < 0 else j) * H
@@ -119,10 +122,10 @@ def tile_multilstm_pa_t_kernel(
             codes, scales = (w_codes[:, cols], w_scales[:, cols]) if j < 0 else (h_codes[:, cols], h_scales[:, cols])
             nc.vector.quantize_mx(out=codes.bitcast(FP8X4), scales=scales, in_=groupeds[j][:])
 
-        def spread(dst, first):
+        def spread(dst, first, eng):
             bank = psum.tile([P, H], F32, name="b_ps", tag="a", bufs=3)
             nc.tensor.matmul(bank[:], lhsT=ones_sq[:], rhs=rows_b[:, first:first + H], start=True, stop=True)
-            nc.scalar.copy(out=dst, in_=bank[:])
+            copy_out(eng, dst, bank[:])
 
         def spread_lnc():
             for i in range(2):
@@ -136,17 +139,17 @@ def tile_multilstm_pa_t_kernel(
             nc.vector.tensor_copy(out=v_t[:], in_=bank[:, 0:48])
             nc.vector.tensor_tensor(out=b_t[:], in0=v_t[:, 16:32], in1=v_t[:, 32:48], op=ALU.add)
 
-        def flip_x(g):
+        def flip_x(g, eng):
             bank = psum.tile([P, 4, P], BF16, name="tp_b", tag="a", bufs=3)
             for i in range(4):
                 nc.tensor.transpose(bank[:, i, :], x_sb[:, 4 * g + i, :], ident_b[:])
-            nc.scalar.copy(out=x_t[:, 4 * g * P:4 * (g + 1) * P], in_=bank[:].rearrange("p t c -> p (t c)"))
+            copy_out(eng, x_t[:, 4 * g * P:4 * (g + 1) * P], bank[:].rearrange("p t c -> p (t c)"))
 
-        def flip_f(dst, src, g):
+        def flip_f(dst, src, g, eng):
             bank = psum.tile([P, 4, P], F32, name="tp_f", tag="a", bufs=3)
             for i in range(4):
                 nc.tensor.transpose(bank[:, i, :], src[:, i, :], ident_f[:])
-            nc.scalar.copy(out=dst[:, 4 * g * P:4 * (g + 1) * P], in_=bank[:].rearrange("p t c -> p (t c)"))
+            copy_out(eng, dst[:, 4 * g * P:4 * (g + 1) * P], bank[:].rearrange("p t c -> p (t c)"))
 
         def gram():
             g_ps = psum.tile([P, P + 2], F32, name="g_ps", tag="a", bufs=3)
@@ -170,8 +173,8 @@ def tile_multilstm_pa_t_kernel(
                 op1=ALU.add,
             )
 
-        def gain():
-            for t in range(16):
+        def gain(g):
+            for t in range(4 * g, 4 * g + 4):
                 nc.gpsimd.tensor_scalar(
                     out=w_s[:, t, :], in0=w_s[:, t, :], scalar1=v_t[:, t:t + 1], scalar2=0.0, op0=ALU.mult, op1=ALU.add
                 )
@@ -215,12 +218,14 @@ def tile_multilstm_pa_t_kernel(
             nc.gpsimd.tensor_tensor(out=rs_a[:, c], in0=ve_a[:, c], in1=mhalf[:, c], op=ALU.pow)
 
         def x_scale(g):
-            xss[g] = small.tile([P, 4, V], F32, name="xs", tag="xs")
+            xss[g] = small.tile([P, 4, V], F32, name="xs", tag="xs", bufs=4)
             for i in range(4):
                 t = 4 * g + i
-                nc.gpsimd.tensor_scalar(
-                    out=xss[g][:, i, :], in0=x_sb[:, t, :], scalar1=rs_a[:, t:t + 1], scalar2=0.0, op0=ALU.mult, op1=ALU.add
-                )
+                dst, src, rs = xss[g][:, i, :], x_sb[:, t, :], rs_a[:, t:t + 1]
+                if i % 2 == 0:
+                    nc.gpsimd.tensor_scalar(out=dst, in0=src, scalar1=rs, scalar2=0.0, op0=ALU.mult, op1=ALU.add)
+                else:
+                    nc.scalar.activation(out=dst, in_=src, func=ACT.Copy, scale=rs)
 
         def fill_r(t, c):
             if not inside(t):
@@ -278,7 +283,8 @@ def tile_multilstm_pa_t_kernel(
                 rs_r[t_r] = rs[:, 0:1]
             if inside(t_c):
                 nc.gpsimd.tensor_scalar(
-                    out=ve[:, 1:2], in0=st_c[t_c][:, 1:2], scalar1=1.0 / H, scalar2=EPS, op0=ALU.mult, op1=ALU.add
+                    out=ve[:, 1:2], in0=st_c[t_c][:, 1:2], scalar1=(1.0 if t_c == NT - 1 else 1.0 / H), scalar2=EPS,
+                    op0=ALU.mult, op1=ALU.add,
                 )
                 rs_c[t_c] = rs[:, 1:2]
             cols = slice(0 if inside(t_r) else 1, 2 if inside(t_c) else 1)
@@ -361,6 +367,13 @@ def tile_multilstm_pa_t_kernel(
                     accum_out=st_c[t][:, 1:2],
                 )
 
+        def cell_stat(t):
+            st6 = small.tile([P, 6], F32, name="st6", tag="st6")
+            nc.vector.bn_stats(out=st6[:], in_=c1s[t][:])
+            mv = small.tile([P, 2], F32, name="mv_c", tag="mv_c")
+            nc.vector.bn_aggr(out=mv[:], in_=st6[:])
+            st_c[t] = mv
+
         def yop(t):
             if inside(t):
                 nc.vector.scalar_tensor_tensor(
@@ -397,31 +410,14 @@ def tile_multilstm_pa_t_kernel(
                 nc.sync.dma_start(out=c0s[s][:], in_=c0_v[:, ST * s:ST * (s + 1), :])
 
         prep = {}
-
-        def put(n, q, job, *args):
-            prep.setdefault((n, q), []).append((job, args))
-
         first = -LEAD - 1
-        put(first, 0, lambda: flip_f(w_f, w_s[:, 4:8, :], 1))
-        put(first, 1, lambda: flip_f(w_f, w_s[:, 0:4, :], 0))
-        put(first, 2, lambda: flip_f(x_f, xss[0][:], 0))
-        put(first, 3, lambda: flip_f(w_f, w_s[:, 8:12, :], 2))
-        put(first + 1, 0, lambda: flip_f(w_f, w_s[:, 12:16, :], 3))
-        put(first + 1, 1, spread_lnc)
-        put(first, 3, pack_half, 1, 0, "a", 3, "s")
-        put(first + 1, 2, pack_half, 1, 1, "a", 3, "s")
-        put(first + 1, 3, quant, 1)
-        for g in range(1, 8):
-            n = ST * (g - 2)
-            put(g - 2, 3, x_scale, g)
-            put(g - 1, 0, lambda g: flip_f(x_f, xss[g][:], g), g)
-            if g > 1:
-                put(n + 1, 0, pack_half, g, 0, "a", 3, "s")
-                put(n + 2, 0, pack_half, g, 1, "a", 3, "s")
-                put(n + 3, 2, quant, g)
-            if g + 1 < 8:
-                put(max(n + 2, first), 1, load_rows, g + 1)
-            put(max(n + 4, first), 2, load_c0, g)
+
+        def put(n, q, job):
+            prep.setdefault((n, q), []).append(job)
+
+        for g in range(2, 8):
+            put(ST * (g - 2) + 4, 2, lambda g=g: load_c0(g))
+        put(first, 0, spread_lnc)
 
         def slot(n):
             for q in range(4):
@@ -430,9 +426,9 @@ def tile_multilstm_pa_t_kernel(
                 if q == 0:
                     scale_r(n + LEAD, 2)
                     scale_r(n + LEAD, 3)
-                    act(t_z, CHUNK_ORDER[q_z])
                     cell_dev(n - 2)
-                    hyop(n - 3, nc.gpsimd)
+                    act(t_z, CHUNK_ORDER[q_z])
+                    c2op(n - 1, nc.gpsimd)
                     rsqrt(n + LEAD, n - 2)
                 elif q == 1:
                     fill_r(n + LEAD + 1, 2)
@@ -442,7 +438,7 @@ def tile_multilstm_pa_t_kernel(
                     act(t_z, CHUNK_ORDER[q_z])
                     stat_mean(n + LEAD + 1, 2)
                     stat_mean(n + LEAD + 1, 3)
-                    c2op(n - 1, nc.gpsimd)
+                    csum(n - 1, nc.gpsimd)
                 elif q == 2:
                     fill_r(n + LEAD + 1, 0)
                     fill_r(n + LEAD + 1, 1)
@@ -450,14 +446,14 @@ def tile_multilstm_pa_t_kernel(
                     act(t_z, CHUNK_ORDER[q_z])
                     stat_dev(n + LEAD + 1, 2)
                     stat_dev(n + LEAD + 1, 3)
-                    csum(n - 1, nc.gpsimd)
+                    hyop(n - 3, nc.gpsimd)
                 else:
                     stat_v(n + LEAD + 1, 0)
                     stat_v(n + LEAD + 1, 1)
                     act(t_z, CHUNK_ORDER[q_z])
                     cell_mean(n - 1)
                     th(n - 2)
-                    c1op(n, nc.gpsimd)
+                    c1op(n, nc.vector if n == NT - 1 else nc.gpsimd)
                 fill_a(t_a, CHUNK_ORDER[q_a])
                 z(n, CHUNK_ORDER[q])
                 if q == 2:
@@ -465,56 +461,102 @@ def tile_multilstm_pa_t_kernel(
                     store_cy(n - 2)
                 if q == 3:
                     aggr(n + LEAD + 1)
-                for job, args in prep.get((n, q), []):
-                    job(*args)
+                for job in prep.get((n, q), []):
+                    job()
+
+        def tail():
+            a, b, c = NT - 3, NT - 2, NT - 1
+            cell_dev(b)
+            act(c, CHUNK_ORDER[3])
+            c2op(c, nc.vector)
+            rsqrt(NT, b)
+            hyop(a, nc.gpsimd)
+            csum(c, nc.vector)
+            cell_stat(c)
+            rsqrt(NT, c)
+            yop(b)
+            cyop(b)
+            store_cy(b)
+            th(b)
+            yop(c)
+            cyop(c)
+            store_cy(c)
+            th(c)
+            hyop(b, nc.vector)
+            hyop(c, nc.vector)
 
         with tc.manual_schedule():
+            nc.scalar.activation(out=warm[:], in_=mhalf[:, 0:1], func=ACT.Sigmoid)
+            nc.scalar.dma_start(out=vec[0:16, :], in_=lni_w1.rearrange("(t p) -> t p", p=P))
+            nc.scalar.dma_start(out=vec[16:32, :], in_=lni_b1.rearrange("(t p) -> t p", p=P))
+            nc.scalar.dma_start(out=vec[32:48, :], in_=lnh_b1.rearrange("(t p) -> t p", p=P))
             nc.sync.dma_start(out=w_n[:], in_=wih_v)
             for i in range(2):
                 nc.sync.dma_start(out=x_sb[:, 16 * i:16 * (i + 1), :], in_=x_v[:, 16 * i:16 * (i + 1), :])
-            load_rows(0)
-            load_rows(-2)
-            nc.sync.dma_start(out=vec[0:16, :], in_=lni_w1.rearrange("(t p) -> t p", p=P))
-            nc.sync.dma_start(out=vec[16:32, :], in_=lni_b1.rearrange("(t p) -> t p", p=P))
-            nc.sync.dma_start(out=vec[32:48, :], in_=lnh_b1.rearrange("(t p) -> t p", p=P))
-            for j in (-1, -4, -3):
+            for j in (0, -2, -1, -4, -3):
                 load_rows(j)
             nc.sync.dma_start(out=rows_b[0:1, 0:G], in_=lnh_w1.rearrange("(o g) -> o g", o=1))
             nc.sync.dma_start(out=rows_b[0:1, G:G + H], in_=lnc_w1.rearrange("(o g) -> o g", o=1))
             nc.sync.dma_start(out=rows_b[0:1, G + H:G + 2 * H], in_=lnc_b1.rearrange("(o g) -> o g", o=1))
-            load_rows(1)
-            load_c0(0)
 
-            def pack(j):
-                pack_half(j, 0, "r", 4, "s")
-                pack_half(j, 1, "r", 4, "v")
-                quant(j)
+            def pack(j, a, b, tag):
+                pack_half(j, 0, tag, 4 if tag == "r" else 3, a)
+                pack_half(j, 1, tag, 4 if tag == "r" else 3, b)
 
+            order = (0, -2, -1, -4, -3, 1, 2, 3, 4, 5, 6, 7)
             gram()
+            flip_x(0, "s")
             center()
-            for g in range(4):
-                flip_x(g)
-                a_stat(g)
-            a_finish(0, 4)
-            pack(0)
-            pack(-2)
             vec_t()
-            gain()
-            x_scale(0)
-            flip_x(4)
-            a_stat(4)
-            pack(-1)
-            flip_x(5)
-            a_stat(5)
-            pack(-4)
-            flip_x(6)
-            a_stat(6)
-            pack(-3)
-            for c in (2, 3, 0, 1):
-                spread(wh_bc[:, c * H:(c + 1) * H], c * H)
-            flip_x(7)
-            a_stat(7)
-            a_finish(4, 16)
-            a_finish(16, NT)
-            for n in range(first, NT + DEPTH):
+            flip_x(1, "s")
+            for g in range(4):
+                gain(g)
+            for i, j in enumerate(order):
+                if 8 == i:
+                    slot(first)
+                if 10 == i:
+                    slot(first + 1)
+                if i < 8:
+                    a_stat(i)
+                if i + 2 < 8:
+                    flip_x(i + 2, "s")
+                pack(j, "s", "v" if i in (4, 7, 10) else "s", "r" if i < 8 else "a")
+                if i + 5 < 12:
+                    load_rows(order[i + 5])
+                if i == 6:
+                    load_c0(0)
+                    load_c0(1)
+                if j == -3:
+                    for c in (2, 3, 0, 1):
+                        spread(wh_bc[:, c * H:(c + 1) * H], c * H, "v" if c % 2 else "s")
+                if i > 0:
+                    quant(order[i - 1])
+                if i == 0:
+                    a_finish(0, 4)
+                    x_scale(0)
+                if i == 3:
+                    a_finish(4, 4 * i + 4)
+                if i == 5:
+                    a_finish(4 * 3 + 4, 4 * i + 4)
+                if i == 7:
+                    a_finish(4 * 5 + 4, NT)
+                if i == 3:
+                    flip_f(w_f, w_s[:, 4:8, :], 1, "s")
+                    flip_f(w_f, w_s[:, 0:4, :], 0, "v")
+                if i == 3+1:
+                    flip_f(w_f, w_s[:, 8:12, :], 2, "s")
+                    flip_f(w_f, w_s[:, 12:16, :], 3, "v")
+                    flip_f(x_f, xss[0][:], 0, "s")
+                if i > 3 and i - 3 <= 3:
+                    x_scale(i - 3)
+                if i - 2 > 3 and i - 2 - 3 <= 3:
+                    flip_f(x_f, xss[i - 2 - 3][:], i - 2 - 3, "s")
+                if i >= 8:
+                    x_scale(i - 4)
+                if i >= 9:
+                    flip_f(x_f, xss[i - 5][:], i - 5, "s")
+            flip_f(x_f, xss[7][:], 7, "s")
+            quant(7)
+            for n in range(0, NT):
                 slot(n)
+            tail()

@@ -419,7 +419,7 @@ def tile_multilstm_pa_t_kernel(
             put(ST * (g - 2) + 4, 2, lambda g=g: load_c0(g))
         put(first, 0, spread_lnc)
 
-        def slot(n):
+        def slot(n, with_a=True):
             for q in range(4):
                 t_z, q_z = divmod(4 * n + q - 1, 4)
                 t_a, q_a = divmod(4 * n + q + 2, 4)
@@ -454,7 +454,8 @@ def tile_multilstm_pa_t_kernel(
                     cell_mean(n - 1)
                     th(n - 2)
                     c1op(n, nc.vector if n == NT - 1 else nc.gpsimd)
-                fill_a(t_a, CHUNK_ORDER[q_a])
+                if with_a:
+                    fill_a(t_a, CHUNK_ORDER[q_a])
                 z(n, CHUNK_ORDER[q])
                 if q == 2:
                     cyop(n - 2)
@@ -509,13 +510,13 @@ def tile_multilstm_pa_t_kernel(
             center()
             vec_t()
             flip_x(1, "s")
-            for g in range(4):
-                gain(g)
+            gain(1)
+            gain(0)
             for i, j in enumerate(order):
                 if 8 == i:
                     slot(first)
                 if 10 == i:
-                    slot(first + 1)
+                    slot(first + 1, with_a=False)
                 if i < 8:
                     a_stat(i)
                 if i + 2 < 8:
@@ -533,6 +534,9 @@ def tile_multilstm_pa_t_kernel(
                     quant(order[i - 1])
                 if i == 0:
                     a_finish(0, 4)
+                    gain(2)
+                    gain(3)
+                if i == 1:
                     x_scale(0)
                 if i == 3:
                     a_finish(4, 4 * i + 4)
@@ -540,23 +544,22 @@ def tile_multilstm_pa_t_kernel(
                     a_finish(4 * 3 + 4, 4 * i + 4)
                 if i == 7:
                     a_finish(4 * 5 + 4, NT)
-                if i == 3:
+                if i == 4:
                     flip_f(w_f, w_s[:, 4:8, :], 1, "s")
                     flip_f(w_f, w_s[:, 0:4, :], 0, "v")
-                if i == 3+1:
+                if i == 4+1:
                     flip_f(w_f, w_s[:, 8:12, :], 2, "s")
                     flip_f(w_f, w_s[:, 12:16, :], 3, "v")
                     flip_f(x_f, xss[0][:], 0, "s")
-                if i > 3 and i - 3 <= 3:
-                    x_scale(i - 3)
-                if i - 2 > 3 and i - 2 - 3 <= 3:
-                    flip_f(x_f, xss[i - 2 - 3][:], i - 2 - 3, "s")
-                if i >= 8:
-                    x_scale(i - 4)
-                if i >= 9:
-                    flip_f(x_f, xss[i - 5][:], i - 5, "s")
-            flip_f(x_f, xss[7][:], 7, "s")
+                for g in range(1, 8):
+                    if i == (0,5,5,6,7,8,9,10)[g]:
+                        x_scale(g)
+                    if i == (2,7,7,8,9,10,11,11)[g]:
+                        flip_f(x_f, xss[g][:], g, "s")
             quant(7)
+            for q in range(2):
+                fill_a(0, CHUNK_ORDER[q])
+
             for n in range(0, NT):
                 slot(n)
             tail()

@@ -395,12 +395,12 @@ def tile_multilstm_pa_t_kernel(
 
         def th(t):
             if inside(t):
-                tcs[t] = work.tile([P, H], F32, name="tcy", tag="tcy")
+                tcs[t] = work.tile([P, H], F32, name="tcy", tag="tcy", bufs=3)
                 nc.scalar.activation(out=tcs[t][:], in_=cys[t][:], func=ACT.Tanh)
 
         def hyop(t, eng):
             if inside(t):
-                hy = work.tile([P, H], F32, name="hy", tag="hy")
+                hy = work.tile([P, H], F32, name="hy", tag="hy", bufs=4)
                 eng.tensor_tensor(out=hy[:], in0=so[t][:], in1=tcs[t][:], op=ALU.mult)
                 nc.sync.dma_start(out=hy_v[:, t, :], in_=hy[:])
 
@@ -426,6 +426,7 @@ def tile_multilstm_pa_t_kernel(
                 if q == 0:
                     scale_r(n + LEAD, 2)
                     scale_r(n + LEAD, 3)
+                    th(n - 3)
                     cell_dev(n - 2)
                     act(t_z, CHUNK_ORDER[q_z])
                     c2op(n - 1, nc.gpsimd)
@@ -452,21 +453,20 @@ def tile_multilstm_pa_t_kernel(
                     stat_v(n + LEAD + 1, 1)
                     act(t_z, CHUNK_ORDER[q_z])
                     cell_mean(n - 1)
-                    th(n - 2)
                     c1op(n, nc.vector if n == NT - 1 else nc.gpsimd)
                 if with_a:
                     fill_a(t_a, CHUNK_ORDER[q_a])
                 z(n, CHUNK_ORDER[q])
-                if q == 2:
-                    cyop(n - 2)
-                    store_cy(n - 2)
                 if q == 3:
                     aggr(n + LEAD + 1)
+                    cyop(n - 2)
+                    store_cy(n - 2)
                 for job in prep.get((n, q), []):
                     job()
 
         def tail():
             a, b, c = NT - 3, NT - 2, NT - 1
+            th(a)
             cell_dev(b)
             act(c, CHUNK_ORDER[3])
             c2op(c, nc.vector)

@@ -74,7 +74,8 @@ def tile_multilstm_pa_t_kernel(
         w_s = const.tile([P, 16, V], F32, name="w_s")
         vec = const.tile([P, P], BF16, name="vec")
         nc.vector.memset(vec[:], 0.0)
-        rows_b = const.tile([P, G + 2 * H], BF16, name="rows_b")
+        rows_b = const.tile([P, G + 3 * H], BF16, name="rows_b")
+        bo_bc = const.tile([P, H], F32, name="bo_bc")
         nc.gpsimd.memset(rows_b[:], 0.0)
         st_r = []
         for i in range(3):
@@ -277,14 +278,12 @@ def tile_multilstm_pa_t_kernel(
             ve = small.tile([P, 2], F32, name="ve", tag="ve")
             rs = small.tile([P, 2], F32, name="rs", tag="rs", bufs=LEAD + 3)
             if inside(t_r):
-                nc.gpsimd.tensor_scalar(
-                    out=ve[:, 0:1], in0=mv_r[t_r][:, 1:2], scalar1=1.0, scalar2=EPS, op0=ALU.mult, op1=ALU.add
-                )
+                nc.scalar.activation(out=ve[:, 0:1], in_=mv_r[t_r][:, 1:2], func=ACT.Copy, bias=EPS)
                 rs_r[t_r] = rs[:, 0:1]
             if inside(t_c):
-                nc.gpsimd.tensor_scalar(
-                    out=ve[:, 1:2], in0=st_c[t_c][:, 1:2], scalar1=(1.0 if t_c == NT - 1 else 1.0 / H), scalar2=EPS,
-                    op0=ALU.mult, op1=ALU.add,
+                nc.scalar.activation(
+                    out=ve[:, 1:2], in_=st_c[t_c][:, 1:2], func=ACT.Copy, bias=EPS,
+                    scale=(1.0 if t_c == NT - 1 else 1.0 / H),
                 )
                 rs_c[t_c] = rs[:, 1:2]
             cols = slice(0 if inside(t_r) else 1, 2 if inside(t_c) else 1)
@@ -302,14 +301,23 @@ def tile_multilstm_pa_t_kernel(
                 op0=ALU.subtract, op1=ALU.mult,
             )
 
+        def by_add(t, c):
+            return c == 3 and t % 2 in (0,)
+
+        def add_bias(t, c):
+            if inside(t) and by_add(t, c):
+                dst = gt[t][:, c * H:(c + 1) * H]
+                nc.gpsimd.tensor_tensor(out=dst, in0=dst, in1=bo_bc[:], op=ALU.add)
+
         def fill_a(t, c):
             if not inside(t):
                 return
             bank = psum.tile([P, H], F32, name="a_ps", tag="a", bufs=3)
             nc.tensor.matmul(
-                bank[:], lhsT=x_f[:, t * P:(t + 1) * P], rhs=w_f[:, c * H:(c + 1) * H], start=True, stop=False
+                bank[:], lhsT=x_f[:, t * P:(t + 1) * P], rhs=w_f[:, c * H:(c + 1) * H],
+                start=True, stop=by_add(t, c),
             )
-            for jb in range(4):
+            for jb in range(0 if by_add(t, c) else 4):
                 col = 4 * c + jb
                 nc.tensor.matmul(
                     bank[:, jb * P:(jb + 1) * P],
@@ -428,7 +436,9 @@ def tile_multilstm_pa_t_kernel(
                     scale_r(n + LEAD, 3)
                     th(n - 3)
                     cell_dev(n - 2)
-                    act(t_z, CHUNK_ORDER[q_z])
+                    add_bias(t_z, CHUNK_ORDER[q_z])
+                    if not by_add(t_z, CHUNK_ORDER[q_z]):
+                        act(t_z, CHUNK_ORDER[q_z])
                     c2op(n - 1, nc.gpsimd)
                     rsqrt(n + LEAD, n - 2)
                 elif q == 1:
@@ -437,6 +447,8 @@ def tile_multilstm_pa_t_kernel(
                     scale_r(n + LEAD, 0)
                     scale_r(n + LEAD, 1)
                     act(t_z, CHUNK_ORDER[q_z])
+                    if by_add(n - 1, CHUNK_ORDER[3]):
+                        act(n - 1, CHUNK_ORDER[3])
                     stat_mean(n + LEAD + 1, 2)
                     stat_mean(n + LEAD + 1, 3)
                     csum(n - 1, nc.gpsimd)
@@ -468,6 +480,7 @@ def tile_multilstm_pa_t_kernel(
             a, b, c = NT - 3, NT - 2, NT - 1
             th(a)
             cell_dev(b)
+            add_bias(c, CHUNK_ORDER[3])
             act(c, CHUNK_ORDER[3])
             c2op(c, nc.vector)
             rsqrt(NT, b)
@@ -499,6 +512,8 @@ def tile_multilstm_pa_t_kernel(
             nc.sync.dma_start(out=rows_b[0:1, 0:G], in_=lnh_w1.rearrange("(o g) -> o g", o=1))
             nc.sync.dma_start(out=rows_b[0:1, G:G + H], in_=lnc_w1.rearrange("(o g) -> o g", o=1))
             nc.sync.dma_start(out=rows_b[0:1, G + H:G + 2 * H], in_=lnc_b1.rearrange("(o g) -> o g", o=1))
+            nc.sync.dma_start(out=rows_b[0:1, G + 2 * H:], in_=lni_b1.rearrange("(o g) -> o g", o=1)[:, 3 * H:])
+            nc.sync.dma_start(out=rows_b[1:2, G + 2 * H:], in_=lnh_b1.rearrange("(o g) -> o g", o=1)[:, 3 * H:])
 
             def pack(j, a, b, tag):
                 pack_half(j, 0, tag, 4 if tag == "r" else 3, a)
@@ -530,6 +545,7 @@ def tile_multilstm_pa_t_kernel(
                 if j == -3:
                     for c in (2, 3, 0, 1):
                         spread(wh_bc[:, c * H:(c + 1) * H], c * H, "v" if c % 2 else "s")
+                    spread(bo_bc[:], G + 2 * H, "v")
                 if i > 0:
                     quant(order[i - 1])
                 if i == 0:

from contextlib import ExitStack

import concourse.mybir as mybir
from concourse.masks import make_identity

F32 = mybir.dt.float32
BF16 = mybir.dt.bfloat16
U32 = mybir.dt.uint32
U8 = mybir.dt.uint8
FP8X4 = mybir.dt.float8_e4m3fn_x4
ALU = mybir.AluOpType
ACT = mybir.ActivationFunctionType

P = 128
B, V, H = 4096, 128, 512
G = 4 * H
NT = B // P
ST = 4
EPS = 1e-5
FLOPS = 2 * B * G * (H + V)
CHUNK_ORDER = (1, 0, 2, 3)
LEAD = 1


def tile_multilstm_pa_t_kernel(
    tc, x, h0, c0, w_ih1, w_hh1, lni_w1, lni_b1, lnh_w1, lnh_b1, lnc_w1, lnc_b1, out_0, out_1
):
    nc = tc.nc
    x_v = x.rearrange("(p t) v -> p t v", t=NT)
    h0_v = h0.rearrange("(p t) k -> p t k", t=NT)
    c0_v = c0.rearrange("(p t) k -> p t k", t=NT)
    hy_v = out_0.rearrange("(p t) k -> p t k", t=NT)
    cy_v = out_1.rearrange("(p t) k -> p t k", t=NT)
    whh_v = w_hh1.rearrange("(t p) k -> p t k", p=P)
    wih_v = w_ih1.rearrange("(t p) v -> p t v", p=P)

    with ExitStack() as ctx:
        const = ctx.enter_context(tc.tile_pool(name="const", bufs=1))
        small = ctx.enter_context(tc.tile_pool(name="small", bufs=2))
        work = ctx.enter_context(tc.tile_pool(name="work", bufs=2))
        psum = ctx.enter_context(tc.psum_pool(name="psum", bufs=4))

        ident_f = const.tile([P, P], F32, name="ident_f")
        make_identity(nc, ident_f[:])
        ident_b = const.tile([P, P], BF16, name="ident_b")
        make_identity(nc, ident_b[:])
        mhalf = const.tile([P, NT], F32, name="mhalf")
        nc.vector.memset(mhalf[:], -0.5)
        ones_b = const.tile([P, 2], BF16, name="ones_b")
        nc.vector.memset(ones_b[:], 1.0)
        ones_sq = const.tile([P, P], BF16, name="ones_sq")
        nc.vector.memset(ones_sq[:], 1.0)

        w_codes = const.tile([P, G], U32, name="w_codes", align_bytes=64)
        w_scales = const.tile([P, G], U8, name="w_scales", align_bytes=64)
        h_codes = const.tile([P, B], U32, name="h_codes", align_bytes=64)
        h_scales = const.tile([P, B], U8, name="h_scales", align_bytes=64)
        x_t = const.tile([P, B], BF16, name="x_t")
        x_f = const.tile([P, B], F32, name="x_f")
        w_f = const.tile([P, G], F32, name="w_f")
        wh_bc = const.tile([P, G], BF16, name="wh_bc")
        g_hl = const.tile([P, 2, P + 2], BF16, name="g_hl")
        v_t = const.tile([P, 48], F32, name="v_t")
        b_t = const.tile([P, 16], F32, name="b_t")
        sum_a = const.tile([P, NT], F32, name="sum_a")
        sumsq_a = const.tile([P, NT], F32, name="sumsq_a")
        mu_a = const.tile([P, NT], F32, name="mu_a")
        musq_a = const.tile([P, NT], F32, name="musq_a")
        var_a = const.tile([P, NT], F32, name="var_a")
        ve_a = const.tile([P, NT], F32, name="ve_a")
        rs_a = const.tile([P, NT], F32, name="rs_a")
        x_sb = const.tile([P, NT, V], BF16, name="x_sb")
        w_n = const.tile([P, 16, V], BF16, name="w_n")
        w_s = const.tile([P, 16, V], F32, name="w_s")
        vec = const.tile([P, P], BF16, name="vec")
        nc.vector.memset(vec[:], 0.0)
        rows_b = const.tile([P, G + 3 * H], BF16, name="rows_b")
        bo_bc = const.tile([P, H], F32, name="bo_bc")
        nc.gpsimd.memset(rows_b[:], 0.0)
        st_r = []
        for i in range(3):
            st = const.tile([P, 18], F32, name="st_r%d" % i)
            nc.vector.memset(st[:], float(H))
            st_r.append(st)
        lnc_bank = psum.tile([P, 2, H], BF16, name="lnc_ps", tag="c", bufs=1)
        warm = const.tile([P, 1], F32, name="warm")

        r_bank, a_bank, y_bank = {}, {}, {}
        gt, so, mv_r, rs_r, c0s = {}, {}, {}, {}, {}
        c1s, c2s, cys, tcs, st_c, rs_c = {}, {}, {}, {}, {}, {}
        raws, groupeds, xss = {}, {}, {}

        def inside(i):
            return 0 <= i < NT

        def copy_out(eng, dst, src):
            if eng == "v":
                nc.vector.tensor_copy(out=dst, in_=src)
            else:
                nc.scalar.copy(out=dst, in_=src)

        def load_rows(j):
            src = whh_v[:, ST * (j + 4):ST * (j + 5), :] if j < 0 else h0_v[:, ST * j:ST * (j + 1), :]
            raws[j] = work.tile([P, ST * H], BF16, name="raw", tag="raw", bufs=5)
            nc.sync.dma_start(out=raws[j][:].rearrange("p (t k) -> p t k", t=ST), in_=src)

        def pack_half(j, half, tag, bufs, eng):
            words = raws[j][:].bitcast(F32)
            if half == 0:
                groupeds[j] = work.tile([P, ST * P * 4], BF16, name="grouped", tag="grouped", bufs=3, align_bytes=64)
            g_words = groupeds[j][:].bitcast(F32).rearrange("p (t c u) -> p t c u", t=ST, u=2)
            bank = psum.tile([P, 2, 2, P], F32, name="tp_w", tag=tag, bufs=bufs)
            for i in range(2):
                for u in range(2):
                    first = (2 * half + i) * (H // 2)
                    nc.tensor.transpose(bank[:, i, u, :], words[:, first + u:first + H // 2:2], ident_f[:])
            dst, src = g_words[:, 2 * half:2 * half + 2, :, :], bank[:].rearrange("p t u c -> p t c u")
            copy_out(eng, dst, src)

        def quant(j):
            first = (j + 4 if j < 0 else j) * H
            cols = slice(first, first + H)
            codes, scales = (w_codes[:, cols], w_scales[:, cols]) if j < 0 else (h_codes[:, cols], h_scales[:, cols])
            nc.vector.quantize_mx(out=codes.bitcast(FP8X4), scales=scales, in_=groupeds[j][:])

        def spread(dst, first, eng):
            bank = psum.tile([P, H], F32, name="b_ps", tag="a", bufs=3)
            nc.tensor.matmul(bank[:], lhsT=ones_sq[:], rhs=rows_b[:, first:first + H], start=True, stop=True)
            copy_out(eng, dst, bank[:])

        def spread_lnc():
            for i in range(2):
                nc.tensor.matmul(
                    lnc_bank[:, i, :], lhsT=ones_sq[:], rhs=rows_b[:, G + i * H:G + (i + 1) * H], start=True, stop=True
                )

        def vec_t():
            bank = psum.tile([P, P], BF16, name="tp_v", tag="a", bufs=3)
            nc.tensor.transpose(bank[:], vec[:], ident_b[:])
            nc.vector.tensor_copy(out=v_t[:], in_=bank[:, 0:48])
            nc.vector.tensor_tensor(out=b_t[:], in0=v_t[:, 16:32], in1=v_t[:, 32:48], op=ALU.add)

        def flip_x(g, eng):
            bank = psum.tile([P, 4, P], BF16, name="tp_b", tag="a", bufs=3)
            for i in range(4):
                nc.tensor.transpose(bank[:, i, :], x_sb[:, 4 * g + i, :], ident_b[:])
            copy_out(eng, x_t[:, 4 * g * P:4 * (g + 1) * P], bank[:].rearrange("p t c -> p (t c)"))

        def flip_f(dst, src, g, eng):
            bank = psum.tile([P, 4, P], F32, name="tp_f", tag="a", bufs=3)
            for i in range(4):
                nc.tensor.transpose(bank[:, i, :], src[:, i, :], ident_f[:])
            copy_out(eng, dst[:, 4 * g * P:4 * (g + 1) * P], bank[:].rearrange("p t c -> p (t c)"))

        def gram():
            g_ps = psum.tile([P, P + 2], F32, name="g_ps", tag="a", bufs=3)
            for t in range(16):
                nc.tensor.matmul(g_ps[:, 0:P], lhsT=w_n[:, t, :], rhs=w_n[:, t, :], start=(t == 0), stop=(t == 15))
            for t in range(16):
                nc.tensor.matmul(g_ps[:, P:P + 2], lhsT=w_n[:, t, :], rhs=ones_b[:], start=(t == 0), stop=(t == 15))
            nc.vector.tensor_copy(out=g_hl[:, 0, :], in_=g_ps[:])
            nc.vector.tensor_tensor(out=g_hl[:, 1, :], in0=g_ps[:], in1=g_hl[:, 0, :], op=ALU.subtract)

        def center():
            bank = psum.tile([P, V], F32, name="m_ps", tag="a", bufs=3)
            for t in range(16):
                nc.tensor.matmul(bank[:], lhsT=ones_sq[:], rhs=w_n[:, t, :], start=(t == 0), stop=(t == 15))
            nc.vector.scalar_tensor_tensor(
                out=w_s[:],
                in0=bank[:].unsqueeze(1).to_broadcast([P, 16, V]),
                scalar=-1.0 / G,
                in1=w_n[:],
                op0=ALU.mult,
                op1=ALU.add,
            )

        def gain(g):
            for t in range(4 * g, 4 * g + 4):
                nc.gpsimd.tensor_scalar(
                    out=w_s[:, t, :], in0=w_s[:, t, :], scalar1=v_t[:, t:t + 1], scalar2=0.0, op0=ALU.mult, op1=ALU.add
                )

        def a_mm(t0):
            y_ps = psum.tile([P, 2, P + 2], F32, name="y_ps", tag="a", bufs=3)
            for i in range(2):
                lhs = x_t[:, (t0 + i) * P:(t0 + i + 1) * P]
                nc.tensor.matmul(y_ps[:, i, :], lhsT=lhs, rhs=g_hl[:, 0, :], start=True, stop=False)
                nc.tensor.matmul(y_ps[:, i, :], lhsT=lhs, rhs=g_hl[:, 1, :], start=False, stop=True)
            y_bank[t0] = y_ps

        def a_red(t0):
            y_ps = y_bank[t0]
            for i in range(2):
                junk = small.tile([P, P], F32, name="junk", tag="junk")
                nc.vector.scalar_tensor_tensor(
                    out=junk[:],
                    in0=y_ps[:, i, 0:P],
                    scalar=1.0,
                    in1=x_sb[:, t0 + i, :],
                    op0=ALU.mult,
                    op1=ALU.mult,
                    accum_out=sumsq_a[:, t0 + i:t0 + i + 1],
                )
            nc.vector.tensor_copy(out=sum_a[:, t0:t0 + 2], in_=y_ps[:, :, P])

        def a_stat(g):
            for t0 in (4 * g, 4 * g + 2):
                a_mm(t0)
                a_red(t0)

        def a_finish(lo, hi):
            c = slice(lo, hi)
            nc.vector.tensor_scalar(out=mu_a[:, c], in0=sum_a[:, c], scalar1=1.0 / G, scalar2=None, op0=ALU.mult)
            nc.vector.tensor_tensor(out=musq_a[:, c], in0=mu_a[:, c], in1=mu_a[:, c], op=ALU.mult)
            nc.vector.scalar_tensor_tensor(
                out=var_a[:, c], in0=sumsq_a[:, c], scalar=1.0 / G, in1=musq_a[:, c], op0=ALU.mult, op1=ALU.subtract
            )
            nc.vector.tensor_scalar(out=ve_a[:, c], in0=var_a[:, c], scalar1=0.0, scalar2=EPS, op0=ALU.max, op1=ALU.add)
            nc.gpsimd.tensor_tensor(out=rs_a[:, c], in0=ve_a[:, c], in1=mhalf[:, c], op=ALU.pow)

        def x_scale(g):
            xss[g] = small.tile([P, 4, V], F32, name="xs", tag="xs", bufs=4)
            for i in range(4):
                t = 4 * g + i
                dst, src, rs = xss[g][:, i, :], x_sb[:, t, :], rs_a[:, t:t + 1]
                if i % 2 == 0:
                    nc.gpsimd.tensor_scalar(out=dst, in0=src, scalar1=rs, scalar2=0.0, op0=ALU.mult, op1=ALU.add)
                else:
                    nc.scalar.activation(out=dst, in_=src, func=ACT.Copy, scale=rs)

        def fill_r(t, c):
            if not inside(t):
                return
            rows = slice(t * P, (t + 1) * P)
            cols = slice(c * H, (c + 1) * H)
            bank = psum.tile([P, H], F32, name="r_ps", tag="r", bufs=4)
            nc.tensor.matmul_mx(
                out=bank[:],
                lhsT=h_codes[:, rows].bitcast(FP8X4),
                lhsT_scale=h_scales[:, rows],
                rhs=w_codes[:, cols].bitcast(FP8X4),
                rhs_scale=w_scales[:, cols],
                start=True,
                stop=True,
            )
            r_bank[(t, c)] = bank

        def stat_v(t, c):
            if inside(t):
                nc.vector.bn_stats(out=st_r[t % 3][:, 6 * c:6 * c + 6], in_=r_bank[(t, c)][:])

        def junk_b():
            return small.tile([P, H], BF16, name="junk_b", tag="junk_b")

        def stat_mean(t, c):
            if inside(t):
                col = 12 + 3 * (c - 2)
                nc.scalar.activation(
                    out=junk_b()[:], in_=r_bank[(t, c)][:], func=ACT.Identity, scale=1.0 / H,
                    accum_out=st_r[t % 3][:, col + 1:col + 2],
                )

        def stat_dev(t, c):
            if inside(t):
                col = 12 + 3 * (c - 2)
                st = st_r[t % 3]
                nc.scalar.activation(
                    out=junk_b()[:], in_=r_bank[(t, c)][:], func=ACT.Square, scale=-1.0,
                    bias=st[:, col + 1:col + 2], accum_out=st[:, col + 2:col + 3],
                )

        def aggr(t):
            if inside(t):
                mv_r[t] = small.tile([P, 2], F32, name="mv_r", tag="mv_r", bufs=3)
                nc.vector.bn_aggr(out=mv_r[t][:], in_=st_r[t % 3][:])

        def rsqrt(t_r, t_c):
            ve = small.tile([P, 2], F32, name="ve", tag="ve")
            rs = small.tile([P, 2], F32, name="rs", tag="rs", bufs=LEAD + 3)
            if inside(t_r):
                nc.scalar.activation(out=ve[:, 0:1], in_=mv_r[t_r][:, 1:2], func=ACT.Copy, bias=EPS)
                rs_r[t_r] = rs[:, 0:1]
            if inside(t_c):
                nc.scalar.activation(
                    out=ve[:, 1:2], in_=st_c[t_c][:, 1:2], func=ACT.Copy, bias=EPS,
                    scale=(1.0 if t_c == NT - 1 else 1.0 / H),
                )
                rs_c[t_c] = rs[:, 1:2]
            cols = slice(0 if inside(t_r) else 1, 2 if inside(t_c) else 1)
            if inside(t_r) or inside(t_c):
                nc.gpsimd.tensor_tensor(out=rs[:, cols], in0=ve[:, cols], in1=mhalf[:, cols], op=ALU.pow)

        def scale_r(t, c):
            if not inside(t):
                return
            if t not in gt:
                gt[t] = work.tile([P, G], F32, name="gate", tag="gate", bufs=LEAD + 4)
            cols = slice(c * H, (c + 1) * H)
            nc.vector.scalar_tensor_tensor(
                out=gt[t][:, cols], in0=r_bank[(t, c)][:], scalar=mv_r[t][:, 0:1], in1=wh_bc[:, cols],
                op0=ALU.subtract, op1=ALU.mult,
            )

        def by_add(t, c):
            return c == 3 and t % 2 in (0,)

        def add_bias(t, c):
            if inside(t) and by_add(t, c):
                dst = gt[t][:, c * H:(c + 1) * H]
                nc.gpsimd.tensor_tensor(out=dst, in0=dst, in1=bo_bc[:], op=ALU.add)

        def fill_a(t, c):
            if not inside(t):
                return
            bank = psum.tile([P, H], F32, name="a_ps", tag="a", bufs=3)
            nc.tensor.matmul(
                bank[:], lhsT=x_f[:, t * P:(t + 1) * P], rhs=w_f[:, c * H:(c + 1) * H],
                start=True, stop=by_add(t, c),
            )
            for jb in range(0 if by_add(t, c) else 4):
                col = 4 * c + jb
                nc.tensor.matmul(
                    bank[:, jb * P:(jb + 1) * P],
                    lhsT=b_t[:, col:col + 1].to_broadcast([P, P]),
                    rhs=ident_f[:],
                    is_transpose=True,
                    start=False,
                    stop=(jb == 3),
                )
            a_bank[(t, c)] = bank

        def z(t, c):
            if inside(t):
                dst = gt[t][:, c * H:(c + 1) * H]
                nc.vector.scalar_tensor_tensor(
                    out=dst, in0=dst, scalar=rs_r[t], in1=a_bank[(t, c)][:], op0=ALU.mult, op1=ALU.add
                )

        def act(t, c):
            if not inside(t):
                return
            src = gt[t][:, c * H:(c + 1) * H]
            if c == 3:
                so[t] = work.tile([P, H], F32, name="so", tag="so", bufs=4)
                nc.scalar.activation(out=so[t][:], in_=src, func=ACT.Sigmoid)
            else:
                nc.scalar.activation(out=src, in_=src, func=(ACT.Tanh if c == 2 else ACT.Sigmoid))

        def c1op(t, eng):
            if inside(t):
                s, bt = divmod(t, ST)
                c1s[t] = work.tile([P, H], F32, name="c1", tag="c1", bufs=4)
                eng.tensor_tensor(out=c1s[t][:], in0=gt[t][:, H:2 * H], in1=c0s[s][:, bt, :], op=ALU.mult)

        def c2op(t, eng):
            if inside(t):
                c2s[t] = work.tile([P, H], F32, name="c2", tag="c2")
                eng.tensor_tensor(out=c2s[t][:], in0=gt[t][:, 0:H], in1=gt[t][:, 2 * H:3 * H], op=ALU.mult)

        def csum(t, eng):
            if inside(t):
                eng.tensor_tensor(out=c1s[t][:], in0=c1s[t][:], in1=c2s[t][:], op=ALU.add)

        def cell_mean(t):
            if inside(t):
                st_c[t] = small.tile([P, 2], F32, name="st_c", tag="st_c", bufs=3)
                nc.scalar.activation(
                    out=junk_b()[:], in_=c1s[t][:], func=ACT.Identity, scale=1.0 / H, accum_out=st_c[t][:, 0:1]
                )

        def cell_dev(t):
            if inside(t):
                nc.scalar.activation(
                    out=junk_b()[:], in_=c1s[t][:], func=ACT.Square, scale=-1.0, bias=st_c[t][:, 0:1],
                    accum_out=st_c[t][:, 1:2],
                )

        def cell_stat(t):
            st6 = small.tile([P, 6], F32, name="st6", tag="st6")
            nc.vector.bn_stats(out=st6[:], in_=c1s[t][:])
            mv = small.tile([P, 2], F32, name="mv_c", tag="mv_c")
            nc.vector.bn_aggr(out=mv[:], in_=st6[:])
            st_c[t] = mv

        def yop(t):
            if inside(t):
                nc.vector.scalar_tensor_tensor(
                    out=c1s[t][:], in0=c1s[t][:], scalar=st_c[t][:, 0:1], in1=lnc_bank[:, 0, :],
                    op0=ALU.subtract, op1=ALU.mult,
                )

        def cyop(t):
            if inside(t):
                cys[t] = work.tile([P, H], F32, name="cy", tag="cy", bufs=3)
                nc.vector.scalar_tensor_tensor(
                    out=cys[t][:], in0=c1s[t][:], scalar=rs_c[t], in1=lnc_bank[:, 1, :],
                    op0=ALU.mult, op1=ALU.add,
                )

        def store_cy(t):
            if inside(t):
                nc.sync.dma_start(out=cy_v[:, t, :], in_=cys[t][:])

        def th(t):
            if inside(t):
                tcs[t] = work.tile([P, H], F32, name="tcy", tag="tcy", bufs=3)
                nc.scalar.activation(out=tcs[t][:], in_=cys[t][:], func=ACT.Tanh)

        def hyop(t, eng):
            if inside(t):
                hy = work.tile([P, H], F32, name="hy", tag="hy", bufs=4)
                eng.tensor_tensor(out=hy[:], in0=so[t][:], in1=tcs[t][:], op=ALU.mult)
                nc.sync.dma_start(out=hy_v[:, t, :], in_=hy[:])

        def load_c0(s):
            if 0 <= s < NT // ST:
                c0s[s] = work.tile([P, ST, H], BF16, name="c0_sb", tag="c0_sb", bufs=2)
                nc.sync.dma_start(out=c0s[s][:], in_=c0_v[:, ST * s:ST * (s + 1), :])

        prep = {}
        first = -LEAD - 1

        def put(n, q, job):
            prep.setdefault((n, q), []).append(job)

        for g in range(2, 8):
            put(ST * (g - 2) + 4, 2, lambda g=g: load_c0(g))
        put(first, 0, spread_lnc)

        def slot(n, with_a=True):
            for q in range(4):
                t_z, q_z = divmod(4 * n + q - 1, 4)
                t_a, q_a = divmod(4 * n + q + 2, 4)
                if q == 0:
                    scale_r(n + LEAD, 2)
                    scale_r(n + LEAD, 3)
                    th(n - 3)
                    cell_dev(n - 2)
                    add_bias(t_z, CHUNK_ORDER[q_z])
                    if not by_add(t_z, CHUNK_ORDER[q_z]):
                        act(t_z, CHUNK_ORDER[q_z])
                    c2op(n - 1, nc.gpsimd)
                    rsqrt(n + LEAD, n - 2)
                elif q == 1:
                    fill_r(n + LEAD + 1, 2)
                    fill_r(n + LEAD + 1, 3)
                    scale_r(n + LEAD, 0)
                    scale_r(n + LEAD, 1)
                    act(t_z, CHUNK_ORDER[q_z])
                    if by_add(n - 1, CHUNK_ORDER[3]):
                        act(n - 1, CHUNK_ORDER[3])
                    stat_mean(n + LEAD + 1, 2)
                    stat_mean(n + LEAD + 1, 3)
                    csum(n - 1, nc.gpsimd)
                elif q == 2:
                    fill_r(n + LEAD + 1, 0)
                    fill_r(n + LEAD + 1, 1)
                    yop(n - 2)
                    act(t_z, CHUNK_ORDER[q_z])
                    stat_dev(n + LEAD + 1, 2)
                    stat_dev(n + LEAD + 1, 3)
                    hyop(n - 3, nc.gpsimd)
                else:
                    stat_v(n + LEAD + 1, 0)
                    stat_v(n + LEAD + 1, 1)
                    act(t_z, CHUNK_ORDER[q_z])
                    cell_mean(n - 1)
                    c1op(n, nc.vector if n == NT - 1 else nc.gpsimd)
                if with_a:
                    fill_a(t_a, CHUNK_ORDER[q_a])
                z(n, CHUNK_ORDER[q])
                if q == 3:
                    aggr(n + LEAD + 1)
                    cyop(n - 2)
                    store_cy(n - 2)
                for job in prep.get((n, q), []):
                    job()

        def tail():
            a, b, c = NT - 3, NT - 2, NT - 1
            th(a)
            cell_dev(b)
            add_bias(c, CHUNK_ORDER[3])
            act(c, CHUNK_ORDER[3])
            c2op(c, nc.vector)
            rsqrt(NT, b)
            hyop(a, nc.gpsimd)
            csum(c, nc.vector)
            cell_stat(c)
            rsqrt(NT, c)
            yop(b)
            cyop(b)
            store_cy(b)
            th(b)
            yop(c)
            cyop(c)
            store_cy(c)
            th(c)
            hyop(b, nc.vector)
            hyop(c, nc.vector)

        with tc.manual_schedule():
            nc.scalar.activation(out=warm[:], in_=mhalf[:, 0:1], func=ACT.Sigmoid)
            nc.scalar.dma_start(out=vec[0:16, :], in_=lni_w1.rearrange("(t p) -> t p", p=P))
            nc.scalar.dma_start(out=vec[16:32, :], in_=lni_b1.rearrange("(t p) -> t p", p=P))
            nc.scalar.dma_start(out=vec[32:48, :], in_=lnh_b1.rearrange("(t p) -> t p", p=P))
            nc.sync.dma_start(out=w_n[:], in_=wih_v)
            for i in range(2):
                nc.sync.dma_start(out=x_sb[:, 16 * i:16 * (i + 1), :], in_=x_v[:, 16 * i:16 * (i + 1), :])
            for j in (0, -2, -1, -4, -3):
                load_rows(j)
            nc.sync.dma_start(out=rows_b[0:1, 0:G], in_=lnh_w1.rearrange("(o g) -> o g", o=1))
            nc.sync.dma_start(out=rows_b[0:1, G:G + H], in_=lnc_w1.rearrange("(o g) -> o g", o=1))
            nc.sync.dma_start(out=rows_b[0:1, G + H:G + 2 * H], in_=lnc_b1.rearrange("(o g) -> o g", o=1))
            nc.sync.dma_start(out=rows_b[0:1, G + 2 * H:], in_=lni_b1.rearrange("(o g) -> o g", o=1)[:, 3 * H:])
            nc.sync.dma_start(out=rows_b[1:2, G + 2 * H:], in_=lnh_b1.rearrange("(o g) -> o g", o=1)[:, 3 * H:])

            def pack(j, a, b, tag):
                pack_half(j, 0, tag, 4 if tag == "r" else 3, a)
                pack_half(j, 1, tag, 4 if tag == "r" else 3, b)

            order = (0, -2, -1, -4, -3, 1, 2, 3, 4, 5, 6, 7)
            gram()
            flip_x(0, "s")
            center()
            vec_t()
            flip_x(1, "s")
            gain(1)
            gain(0)
            for i, j in enumerate(order):
                if 8 == i:
                    slot(first)
                if 10 == i:
                    slot(first + 1, with_a=False)
                if i < 8:
                    a_stat(i)
                if i + 2 < 8:
                    flip_x(i + 2, "s")
                pack(j, "s", "v" if i in (4, 7, 10) else "s", "r" if i < 8 else "a")
                if i + 5 < 12:
                    load_rows(order[i + 5])
                if i == 6:
                    load_c0(0)
                    load_c0(1)
                if j == -3:
                    for c in (2, 3, 0, 1):
                        spread(wh_bc[:, c * H:(c + 1) * H], c * H, "v" if c % 2 else "s")
                    spread(bo_bc[:], G + 2 * H, "v")
                if i > 0:
                    quant(order[i - 1])
                if i == 0:
                    a_finish(0, 4)
                    gain(2)
                    gain(3)
                if i == 1:
                    x_scale(0)
                if i == 3:
                    a_finish(4, 4 * i + 4)
                if i == 5:
                    a_finish(4 * 3 + 4, 4 * i + 4)
                if i == 7:
                    a_finish(4 * 5 + 4, NT)
                if i == 4:
                    flip_f(w_f, w_s[:, 4:8, :], 1, "s")
                    flip_f(w_f, w_s[:, 0:4, :], 0, "v")
                if i == 4+1:
                    flip_f(w_f, w_s[:, 8:12, :], 2, "s")
                    flip_f(w_f, w_s[:, 12:16, :], 3, "v")
                    flip_f(x_f, xss[0][:], 0, "s")
                for g in range(1, 8):
                    if i == (0,5,5,6,7,8,9,10)[g]:
                        x_scale(g)
                    if i == (2,7,7,8,9,10,11,11)[g]:
                        flip_f(x_f, xss[g][:], g, "s")
            quant(7)
            for q in range(2):
                fill_a(0, CHUNK_ORDER[q])

            for n in range(0, NT):
                slot(n)
            tail()
